import numpy as np
import ml_dtypes


def mxq(x, axis, fmt="e4m3"):
    dtype, down = {"e4m3": (ml_dtypes.float8_e4m3fn, 7), "e5m2": (ml_dtypes.float8_e5m2, 14)}[fmt]
    v = np.moveaxis(np.asarray(x, np.float32).astype(ml_dtypes.bfloat16).astype(np.float64), axis, -1)
    blocks = v.reshape(v.shape[:-1] + (-1, 32))
    amax = np.abs(blocks).max(-1, keepdims=True)
    byte = np.maximum(np.where(amax > 0, np.frexp(amax)[1] - 1 + 127, 0) - down, 1)
    scale = np.exp2(byte - 127.0)
    codes = (blocks / scale).astype(np.float32).astype(dtype).astype(np.float64)
    return np.moveaxis((codes * scale).reshape(v.shape), -1, axis)


WIDE = False


def mx_kscale(k):
    if not WIDE:
        return np.ones(k)
    levels = np.array([10, -10, 5, -5, 0])
    a = np.random.permutation(np.resize(levels, k // 512 * 4)).reshape(k // 512, 4)
    idx = np.arange(k)
    return np.exp2(a[idx // 512, idx % 128 // 32])


BF16 = ml_dtypes.bfloat16


def bf(x):
    return np.asarray(x, np.float32).astype(BF16)


def f64(x):
    return np.asarray(x).astype(np.float64)


B, LQ, LK, DIN, H = 2, 512, 2048, 1024, 256
FLOOR = 1e-9


def setup_inputs():
    s = mx_kscale(DIN)
    mass = np.where(np.random.random((B, LQ, 1)) < 0.25, FLOOR, 1.0)
    return {"q": bf(np.random.standard_normal((B, LQ, H)) * 1.5),
            "k": bf(np.random.standard_normal((B, LK, H)) * 1.5),
            "v_ret": bf(np.random.standard_normal((B, LK, DIN)) * s),
            "pi_star": bf(mass * np.exp(1.25 * np.random.standard_normal((B, LQ, LK)))),
            "Wv": bf(np.random.standard_normal((DIN, H)) * 1.5 / np.sqrt(DIN) / s[:, None]),
            "bv": bf(np.random.standard_normal(H) * 0.25),
            "gamma": bf(1.25 + 0.25 * np.random.random(1))}


def reference(q, k, v_ret, pi_star, Wv, bv, gamma):
    wvq = mxq(f64(Wv), 0, "e4m3")
    rows = []
    for b in range(B):
        v = (mxq(f64(v_ret[b]), 1, "e4m3") @ wvq) + f64(bv)
        logits = f64(q[b]) @ f64(k[b]).T / np.sqrt(H)
        z = logits + f64(gamma) * np.log(np.maximum(f64(pi_star[b]), FLOOR))
        e = np.exp(z - z.max(1, keepdims=True))
        rows.append((mxq(e, 1, "e4m3") @ mxq(v, 0, "e4m3")) / e.sum(1, keepdims=True))
    return np.stack(rows)

@@ -1,0 +1,380 @@
+from contextlib import ExitStack
+
+import concourse.mybir as mybir
+from concourse.masks import make_identity
+
+FLOPS = 2 * 2 * (2048 * 1024 * 256 + 2 * 512 * 2048 * 256)
+
+BF16 = mybir.dt.bfloat16
+F32 = mybir.dt.float32
+U32 = mybir.dt.uint32
+U8 = mybir.dt.uint8
+FP8X4 = mybir.dt.float8_e4m3fn_x4
+ALU = mybir.AluOpType
+ACT = mybir.ActivationFunctionType
+AX = mybir.AxisListType
+
+P = 128
+B, LQ, LK, DIN, H = 2, 512, 2048, 1024, 256
+FLOOR = 1e-9
+BIG = 3.4e38
+N_TILES = B * LQ // P
+N_CHUNKS = B * LK // 512
+LN_AHEAD = 4
+Z_WHOLE = 2
+Z_EARLY = 3
+
+
+def mark(label):
+    return label
+
+
+def tile_pgwcrossattention_pa_kernel(tc, q, k, v_ret, pi_star, Wv, bv, gamma, out):
+    nc = tc.nc
+    with ExitStack() as ctx:
+        const = ctx.enter_context(tc.tile_pool(name="const", bufs=1))
+        pip = ctx.enter_context(tc.tile_pool(name="pip", bufs=4))
+        lzp = ctx.enter_context(tc.tile_pool(name="lzp", bufs=8))
+        xrp = ctx.enter_context(tc.tile_pool(name="xrp", bufs=4))
+        kqp = ctx.enter_context(tc.tile_pool(name="kqp", bufs=1))
+        ktp = ctx.enter_context(tc.tile_pool(name="ktp", bufs=2))
+        ep = ctx.enter_context(tc.tile_pool(name="ep", bufs=2))
+        ecp = ctx.enter_context(tc.tile_pool(name="ecp", bufs=3))
+        gxp = ctx.enter_context(tc.tile_pool(name="gxp", bufs=3))
+        gvp = ctx.enter_context(tc.tile_pool(name="gvp", bufs=2))
+        vcp = ctx.enter_context(tc.tile_pool(name="vcp", bufs=2))
+        op = ctx.enter_context(tc.tile_pool(name="op", bufs=3))
+        stp = ctx.enter_context(tc.tile_pool(name="stp", bufs=8))
+        ps_acc = ctx.enter_context(tc.psum_pool(name="ps_acc", bufs=5))
+        ps_tp = ctx.enter_context(tc.psum_pool(name="ps_tp", bufs=3))
+        ctx.enter_context(tc.manual_schedule())
+
+        S = {}
+
+        def consts():
+            mark("const")
+            S["idf"] = const.tile([P, P], F32, name="idf")
+            S["idb"] = const.tile([P, P], BF16, name="idb")
+            make_identity(nc, S["idf"][:])
+            make_identity(nc, S["idb"][:])
+            S["gam_b"] = const.tile([P, 1], BF16, name="gam_b")
+            S["gam"] = const.tile([P, 1], F32, name="gam")
+            S["bias"] = const.tile([P, H], BF16, name="bias")
+            nc.scalar.dma_start(out=S["gam_b"][:], in_=gamma.partition_broadcast(P))
+            nc.scalar.dma_start(out=S["bias"][:], in_=bv.partition_broadcast(P))
+            warm = const.tile([P, 1], F32, name="warm")
+            nc.vector.memset(warm[:], 1.0)
+            nc.scalar.activation(out=warm[:], in_=warm[:], func=ACT.Ln)
+            nc.vector.tensor_copy(out=S["gam"][:], in_=S["gam_b"][:])
+
+        def load_pi(t):
+            mark("LP.%d" % t)
+            b, qt = divmod(t, 4)
+            x = pip.tile([P, LK], BF16, name="pi")
+            nc.sync.dma_start(out=x[:], in_=pi_star[b, qt * P:(qt + 1) * P, :])
+            S["pi", t] = x
+
+        def load_q(b):
+            mark("LQ.%d" % b)
+            qr = kqp.tile([P, 4 * H], BF16, name="qr")
+            nc.sync.dma_start(out=qr[:].rearrange("p (t h) -> p t h", h=H), in_=q[b].rearrange("(t p) h -> p t h", p=P))
+            S["qr", b] = qr
+
+        def load_k(b):
+            kr = kqp.tile([P, 16 * H], BF16, name="kr")
+            S["kr", b] = kr
+            for j in range(4):
+                mark("LK.%d.%d" % (b, j))
+                nc.sync.dma_start(out=kr[:, j * 4 * H:(j + 1) * 4 * H].rearrange("p (t h) -> p t h", h=H),
+                                  in_=k[b, j * 512:(j + 1) * 512, :].rearrange("(t p) h -> p t h", p=P))
+
+        def load_w():
+            mark("LW")
+            wr = ep.tile([P, 2048], BF16, name="e")
+            nc.sync.dma_start(out=wr[:].rearrange("p (c x) -> p c x", c=4), in_=Wv.rearrange("(c p e) h -> p c (e h)", p=P, e=2))
+            S["wr"] = wr
+
+        def load_x(c):
+            mark("LX.%d" % c)
+            b, g = divmod(c, 4)
+            xr = xrp.tile([P, 4 * DIN], BF16, name="xr")
+            nc.sync.dma_start(out=xr[:].rearrange("p (t d) -> p t d", t=4),
+                              in_=v_ret[b, g * 512:(g + 1) * 512, :].rearrange("(t p) d -> p t d", p=P))
+            S["xr", c] = xr
+
+        def w_group():
+            mark("WG.g")
+            wg = ep.tile([P, 2048], BF16, name="ge", align_bytes=64)
+            S["wg"] = wg
+            nc.gpsimd.tensor_scalar(out=wg[:].rearrange("p (g h t) -> p g h t", g=2, t=4),
+                                    in0=S["wr"][:].rearrange("p (g t h) -> p g h t", g=2, t=4), scalar1=1.0, scalar2=0.0, op0=ALU.mult, op1=ALU.add)
+
+        def w_quant():
+            mark("WQ")
+            wc = const.tile([P, 512], U32, name="wc", align_bytes=64)
+            ws = const.tile([P, 512], U8, name="ws", align_bytes=64)
+            nc.vector.quantize_mx(out=wc[:].bitcast(FP8X4), scales=ws[:], in_=S["wg"][:])
+            S["wc"], S["ws"] = wc, ws
+
+        def KT(b, j):
+            mark("KT.%d.%d" % (b, j))
+            ps = ps_tp.tile([P, 512], F32, name="tp")
+            S["pk", b, j] = ps
+            src = S["qr", b][:].bitcast(F32) if j == 0 else S["kr", b][:].bitcast(F32)[:, (j - 1) * 512:j * 512]
+            for i in range(4):
+                nc.tensor.transpose(ps[:, i * P:(i + 1) * P], src[:, i * P:(i + 1) * P], S["idf"][:])
+
+        def KE(b, j, eng):
+            mark("KE.%d.%d.%s" % (b, j, eng))
+            ps = S["pk", b, j]
+            if j == 0:
+                qT = ktp.tile([P, 2, LQ], BF16, name="qT")
+                S["qT", b] = qT
+                src2 = ps[:].bitcast(BF16).rearrange("p (q e) -> p e q", e=2)
+                if eng == "v":
+                    nc.vector.tensor_scalar_mul(out=qT[:], in0=src2, scalar1=0.0625)
+                else:
+                    nc.scalar.activation(out=qT[:], in_=src2, func=ACT.Copy, scale=0.0625)
+            else:
+                if j == 1:
+                    S["kT", b] = ktp.tile([P, 2 * LK], BF16, name="kT")
+                dst = S["kT", b][:].bitcast(F32)[:, (j - 1) * 512:j * 512]
+                if eng == "v":
+                    nc.vector.tensor_copy(out=dst, in_=ps[:])
+                else:
+                    nc.scalar.copy(out=dst, in_=ps[:])
+
+        def Fl(t, eng):
+            mark("F.%d.%s" % (t, eng))
+            x = lzp.tile([P, LK], F32, name="lz")
+            S["lz", t] = x
+            if eng == "v":
+                nc.vector.tensor_scalar_max(out=x[:], in0=S["pi", t][:], scalar1=FLOOR)
+            else:
+                nc.gpsimd.tensor_scalar(out=x[:], in0=S["pi", t][:], scalar1=BIG, scalar2=FLOOR, op0=ALU.min, op1=ALU.max)
+
+        def LN(t):
+            mark("LN.%d" % t)
+            x = S["lz", t]
+            nc.scalar.activation(out=x[:], in_=x[:], func=ACT.Ln)
+
+        def LG(t, i):
+            mark("LG.%d.%d" % (t, i))
+            b, qt = divmod(t, 4)
+            lg = ps_acc.tile([P, 512], F32, name="acc")
+            S["lg", t, i] = lg
+            kv = S["kT", b][:].rearrange("p (k e) -> p k e", e=2)
+            for e in range(2):
+                nc.tensor.matmul(lg[:], lhsT=S["qT", b][:, e, qt * P:(qt + 1) * P], rhs=kv[:, i * 512:(i + 1) * 512, e],
+                                 start=(e == 0), stop=(e == 1))
+
+        def Z(t, i):
+            mark("Z.%d.%d" % (t, i))
+            sl = S["lz", t][:, i * 512:(i + 1) * 512]
+            nc.vector.scalar_tensor_tensor(out=sl, in0=sl, scalar=S["gam"][:, 0:1], in1=S["lg", t, i][:], op0=ALU.mult, op1=ALU.add)
+
+        def MR(t):
+            mark("MR.%d" % t)
+            nm = stp.tile([P, 1], F32, name="nm")
+            S["nm", t] = nm
+            nc.vector.tensor_reduce(out=nm[:], in_=S["lz", t][:], axis=AX.X, op=ALU.max, negate=True)
+
+        def EX(t):
+            mark("EX.%d" % t)
+            e = ep.tile([P, LK], BF16, name="e")
+            rs = stp.tile([P, 1], F32, name="rs")
+            S["e", t], S["rs", t] = e, rs
+            nc.scalar.activation(out=e[:], in_=S["lz", t][:], func=ACT.Exp, bias=S["nm", t][:, 0:1], scale=1.0, accum_out=rs[:, 0:1])
+
+        def ET(t, h):
+            mark("ET.%d.%d" % (t, h))
+            pe = ps_tp.tile([P, 1024], BF16, name="tp")
+            S["pe", t, h] = pe
+            for j in range(8):
+                jj = h * 8 + j
+                nc.tensor.transpose(pe[:, j * P:(j + 1) * P], S["e", t][:, jj * P:(jj + 1) * P], S["idb"][:])
+
+        def EV(t, h):
+            mark("EV.%d.%d.s" % (t, h))
+            if h == 0:
+                S["ge", t] = ep.tile([P, 2048], BF16, name="ge", align_bytes=64)
+            dst = S["ge", t][:, h * 1024:(h + 1) * 1024].rearrange("p (g q t) -> p g q t", g=2, t=4)
+            src = S["pe", t, h][:].rearrange("p (g t q) -> p g q t", g=2, t=4)
+            nc.scalar.copy(out=dst, in_=src)
+
+        def QE(t):
+            mark("QE.%d" % t)
+            ec = ecp.tile([P, 512], U32, name="ec", align_bytes=64)
+            es = ecp.tile([P, 512], U8, name="es", align_bytes=64)
+            S["ec", t], S["es", t] = ec, es
+            nc.vector.quantize_mx(out=ec[:].bitcast(FP8X4), scales=es[:], in_=S["ge", t][:])
+            mark("OR.%d" % t)
+            ri = stp.tile([P, 1], F32, name="ri")
+            S["ri", t] = ri
+            nc.vector.reciprocal(out=ri[:], in_=S["rs", t][:])
+
+        def M2(t):
+            mark("M2.%d" % t)
+            b, qt = divmod(t, 4)
+            po = ps_acc.tile([P, H], F32, name="acc")
+            S["po", t] = po
+            for g in range(4):
+                nc.tensor.matmul_mx(po[:], lhsT=S["ec", t][:, g * P:(g + 1) * P].bitcast(FP8X4), lhsT_scale=S["es", t][:, g * P:(g + 1) * P],
+                                    rhs=S["vc", b][:, g * H:(g + 1) * H].bitcast(FP8X4), rhs_scale=S["vs", b][:, g * H:(g + 1) * H],
+                                    start=(g == 0), stop=(g == 3))
+
+        def OM(t):
+            mark("OM.%d.v" % t)
+            b, qt = divmod(t, 4)
+            o = op.tile([P, H], F32, name="o")
+            nc.vector.tensor_scalar_mul(out=o[:], in0=S["po", t][:], scalar1=S["ri", t][:, 0:1])
+            mark("OS.%d" % t)
+            nc.sync.dma_start(out=out[b, qt * P:(qt + 1) * P, :], in_=o[:])
+
+        def XT(c, t):
+            mark("XT.%d.%d" % (c, t))
+            px = ps_tp.tile([P, 512], F32, name="tp")
+            S["px", c, t] = px
+            src = S["xr", c][:].bitcast(F32)
+            for i in range(4):
+                nc.tensor.transpose(px[:, i * P:(i + 1) * P], src[:, t * 512 + i * P:t * 512 + (i + 1) * P], S["idf"][:])
+
+        def XE(c, t):
+            mark("XE.%d.%d.s" % (c, t))
+            if t == 0:
+                S["gx", c] = gxp.tile([P, 4096], BF16, name="gx", align_bytes=64)
+            dst = S["gx", c][:].bitcast(F32)[:, t * 512:(t + 1) * 512].rearrange("p (g k u) -> p g k u", g=2, u=2)
+            src = S["px", c, t][:].rearrange("p (g u k) -> p g k u", g=2, u=2)
+            nc.scalar.copy(out=dst, in_=src)
+
+        def QX(c):
+            mark("QX.%d" % c)
+            xc = gxp.tile([P, 1024], U32, name="xc", align_bytes=64)
+            xs = gxp.tile([P, 1024], U8, name="xs", align_bytes=64)
+            S["xc", c], S["xs", c] = xc, xs
+            nc.vector.quantize_mx(out=xc[:].bitcast(FP8X4), scales=xs[:], in_=S["gx", c][:])
+
+        def M1(c):
+            xc, xs, wc, ws = S["xc", c], S["xs", c], S["wc"], S["ws"]
+            for hh in range(2):
+                mark("M1.%d.%d" % (c, hh))
+                pv = ps_acc.tile([P, 512], F32, name="acc")
+                S["pv", c, hh] = pv
+                for t in range(4):
+                    for gd in range(2):
+                        a = t * 256 + gd * P
+                        w0 = gd * H + hh * P
+                        nc.tensor.matmul_mx(pv[:, t * P:(t + 1) * P], lhsT=xc[:, a:a + P].bitcast(FP8X4), lhsT_scale=xs[:, a:a + P],
+                                            rhs=wc[:, w0:w0 + P].bitcast(FP8X4), rhs_scale=ws[:, w0:w0 + P],
+                                            start=(gd == 0), stop=(gd == 1))
+
+        def VE(c):
+            gv = gvp.tile([P, 1024], BF16, name="gv", align_bytes=64)
+            S["gv", c] = gv
+            for hh in range(2):
+                mark("VE.%d.%d" % (c, hh))
+                nc.vector.tensor_tensor(out=gv[:, hh * 512:(hh + 1) * 512].rearrange("p (h t) -> p h t", t=4),
+                                        in0=S["pv", c, hh][:].rearrange("p (t h) -> p h t", t=4),
+                                        in1=S["bias"][:, hh * P:(hh + 1) * P].unsqueeze(2).to_broadcast([P, P, 4]), op=ALU.add)
+
+        def QV(c):
+            mark("QV.%d" % c)
+            b, g = divmod(c, 4)
+            if g == 0:
+                S["vc", b] = vcp.tile([P, 4 * H], U32, name="vc", align_bytes=64)
+                S["vs", b] = vcp.tile([P, 4 * H], U8, name="vs", align_bytes=64)
+            nc.vector.quantize_mx(out=S["vc", b][:, g * H:(g + 1) * H].bitcast(FP8X4), scales=S["vs", b][:, g * H:(g + 1) * H], in_=S["gv", c][:])
+
+        consts()
+        for t in range(3):
+            load_pi(t)
+        load_q(0)
+        load_pi(3)
+        load_k(0)
+        load_x(0)
+        load_w()
+        for t in range(LN_AHEAD):
+            Fl(t, "v")
+        for t in range(LN_AHEAD):
+            LN(t)
+        for j in range(5):
+            KT(0, j)
+            KE(0, j, "v")
+        for t in range(Z_WHOLE):
+            for i in range(4):
+                LG(t, i)
+            for i in range(4):
+                Z(t, i)
+            MR(t)
+        w_group()
+        w_quant()
+        for t in range(3):
+            XT(0, t)
+
+        K1_PIECES = {4: (0,), 5: (1, 2), 6: (3, 4)}
+        for a in range(N_CHUNKS + 2):
+            if a < N_CHUNKS:
+                if a + LN_AHEAD < N_TILES:
+                    load_pi(a + LN_AHEAD)
+                    Fl(a + LN_AHEAD, "g")
+                if a + 1 < N_CHUNKS:
+                    if a + 1 == 5:
+                        load_q(1)
+                        load_k(1)
+                    load_x(a + 1)
+                XE(a, 0)
+                XT(a, 3)
+                for t in range(1, 4):
+                    XE(a, t)
+                if a + LN_AHEAD < N_TILES:
+                    LN(a + LN_AHEAD)
+                for j in K1_PIECES.get(a, ()):
+                    KT(1, j)
+                    KE(1, j, "s")
+                if a + 1 < N_CHUNKS:
+                    for t in range(3):
+                        XT(a + 1, t)
+            zt = Z_WHOLE
+            if a >= 2:
+                VE(a - 2)
+            if a in (1, 2):
+                for i in (2 * a - 2, 2 * a - 1):
+                    Z(zt, i)
+            if a == 3:
+                MR(zt)
+            if a >= 2:
+                QV(a - 2)
+            if a < N_CHUNKS:
+                QX(a)
+            if 1 <= a <= N_CHUNKS:
+                M1(a - 1)
+            if a + 1 in (1, 2):
+                for i in (2 * a, 2 * a + 1):
+                    LG(zt, i)
+
+        for i in range(4):
+            LG(Z_EARLY, i)
+        EX(0)
+        for r in range(N_TILES + 2):
+            t = Z_EARLY + r
+            if r + 1 < N_TILES:
+                EX(r + 1)
+            if r < N_TILES:
+                ET(r, 0)
+                ET(r, 1)
+                EV(r, 0)
+                EV(r, 1)
+            if 0 <= r - 2:
+                OM(r - 2)
+            if t < N_TILES:
+                for i in range(4):
+                    Z(t, i)
+            if 1 <= r <= N_TILES:
+                QE(r - 1)
+            if t < N_TILES:
+                MR(t)
+            if t + 1 < N_TILES:
+                for i in range(4):
+                    LG(t + 1, i)
+            if 1 <= r <= N_TILES:
+                M2(r - 1)

@@ -22,7 +22,8 @@ N_TILES = B * LQ // P
 N_CHUNKS = B * LK // 512
 LN_AHEAD = 4
 Z_WHOLE = 2
-Z_EARLY = 3
+Z_EARLY = 4
+EV_SHARED = 4
 
 
 def mark(label):
@@ -194,13 +195,16 @@ def tile_pgwcrossattention_pa_kernel(tc, q, k, v_ret, pi_star, Wv, bv, gamma, ou
                 jj = h * 8 + j
                 nc.tensor.transpose(pe[:, j * P:(j + 1) * P], S["e", t][:, jj * P:(jj + 1) * P], S["idb"][:])
 
-        def EV(t, h):
-            mark("EV.%d.%d.s" % (t, h))
+        def EV(t, h, eng):
+            mark("EV.%d.%d.%s" % (t, h, eng))
             if h == 0:
                 S["ge", t] = ep.tile([P, 2048], BF16, name="ge", align_bytes=64)
             dst = S["ge", t][:, h * 1024:(h + 1) * 1024].rearrange("p (g q t) -> p g q t", g=2, t=4)
             src = S["pe", t, h][:].rearrange("p (g t q) -> p g q t", g=2, t=4)
-            nc.scalar.copy(out=dst, in_=src)
+            if eng == "v":
+                nc.vector.tensor_copy(out=dst, in_=src)
+            else:
+                nc.scalar.copy(out=dst, in_=src)
 
         def QE(t):
             mark("QE.%d" % t)
@@ -254,19 +258,18 @@ def tile_pgwcrossattention_pa_kernel(tc, q, k, v_ret, pi_star, Wv, bv, gamma, ou
             S["xc", c], S["xs", c] = xc, xs
             nc.vector.quantize_mx(out=xc[:].bitcast(FP8X4), scales=xs[:], in_=S["gx", c][:])
 
-        def M1(c):
+        def M1(c, hh):
+            mark("M1.%d.%d" % (c, hh))
             xc, xs, wc, ws = S["xc", c], S["xs", c], S["wc"], S["ws"]
-            for hh in range(2):
-                mark("M1.%d.%d" % (c, hh))
-                pv = ps_acc.tile([P, 512], F32, name="acc")
-                S["pv", c, hh] = pv
-                for t in range(4):
-                    for gd in range(2):
-                        a = t * 256 + gd * P
-                        w0 = gd * H + hh * P
-                        nc.tensor.matmul_mx(pv[:, t * P:(t + 1) * P], lhsT=xc[:, a:a + P].bitcast(FP8X4), lhsT_scale=xs[:, a:a + P],
-                                            rhs=wc[:, w0:w0 + P].bitcast(FP8X4), rhs_scale=ws[:, w0:w0 + P],
-                                            start=(gd == 0), stop=(gd == 1))
+            pv = ps_acc.tile([P, 512], F32, name="acc")
+            S["pv", c, hh] = pv
+            for t in range(4):
+                for gd in range(2):
+                    a = t * 256 + gd * P
+                    w0 = gd * H + hh * P
+                    nc.tensor.matmul_mx(pv[:, t * P:(t + 1) * P], lhsT=xc[:, a:a + P].bitcast(FP8X4), lhsT_scale=xs[:, a:a + P],
+                                        rhs=wc[:, w0:w0 + P].bitcast(FP8X4), rhs_scale=ws[:, w0:w0 + P],
+                                        start=(gd == 0), stop=(gd == 1))
 
         def VE(c):
             gv = gvp.tile([P, 1024], BF16, name="gv", align_bytes=64)
@@ -312,6 +315,10 @@ def tile_pgwcrossattention_pa_kernel(tc, q, k, v_ret, pi_star, Wv, bv, gamma, ou
             XT(0, t)
 
         K1_PIECES = {4: (0,), 5: (1, 2), 6: (3, 4)}
+
+        def z_step(a):
+            return divmod(a - 1, 3) if 1 <= a <= 6 else (0, 3)
+
         for a in range(N_CHUNKS + 2):
             if a < N_CHUNKS:
                 if a + LN_AHEAD < N_TILES:
@@ -331,26 +338,29 @@ def tile_pgwcrossattention_pa_kernel(tc, q, k, v_ret, pi_star, Wv, bv, gamma, ou
                 for j in K1_PIECES.get(a, ()):
                     KT(1, j)
                     KE(1, j, "s")
-                if a + 1 < N_CHUNKS:
-                    for t in range(3):
-                        XT(a + 1, t)
-            zt = Z_WHOLE
             if a >= 2:
                 VE(a - 2)
-            if a in (1, 2):
-                for i in (2 * a - 2, 2 * a - 1):
-                    Z(zt, i)
-            if a == 3:
-                MR(zt)
+            zt, step = z_step(a)
+            if step < 2:
+                Z(Z_WHOLE + zt, 2 * step)
+                Z(Z_WHOLE + zt, 2 * step + 1)
+            elif step == 2:
+                MR(Z_WHOLE + zt)
             if a >= 2:
                 QV(a - 2)
             if a < N_CHUNKS:
                 QX(a)
             if 1 <= a <= N_CHUNKS:
-                M1(a - 1)
-            if a + 1 in (1, 2):
-                for i in (2 * a, 2 * a + 1):
-                    LG(zt, i)
+                M1(a - 1, 0)
+            if a + 1 < N_CHUNKS:
+                for t in range(3):
+                    XT(a + 1, t)
+            if 1 <= a <= N_CHUNKS:
+                M1(a - 1, 1)
+            zt, step = z_step(a + 1)
+            if step < 2:
+                LG(Z_WHOLE + zt, 2 * step)
+                LG(Z_WHOLE + zt, 2 * step + 1)
 
         for i in range(4):
             LG(Z_EARLY, i)
@@ -362,8 +372,9 @@ def tile_pgwcrossattention_pa_kernel(tc, q, k, v_ret, pi_star, Wv, bv, gamma, ou
             if r < N_TILES:
                 ET(r, 0)
                 ET(r, 1)
-                EV(r, 0)
-                EV(r, 1)
+                EV(r, 0, "s")
+                if r < EV_SHARED:
+                    EV(r, 1, "s")
             if 0 <= r - 2:
                 OM(r - 2)
             if t < N_TILES:
@@ -373,6 +384,8 @@ def tile_pgwcrossattention_pa_kernel(tc, q, k, v_ret, pi_star, Wv, bv, gamma, ou
                 QE(r - 1)
             if t < N_TILES:
                 MR(t)
+            if EV_SHARED <= r < N_TILES:
+                EV(r, 1, "v")
             if t + 1 < N_TILES:
                 for i in range(4):
                     LG(t + 1, i)

@@ -40,7 +40,7 @@ def tile_pgwcrossattention_pa_kernel(tc, q, k, v_ret, pi_star, Wv, bv, gamma, ou
         kqp = ctx.enter_context(tc.tile_pool(name="kqp", bufs=1))
         ktp = ctx.enter_context(tc.tile_pool(name="ktp", bufs=2))
         ep = ctx.enter_context(tc.tile_pool(name="ep", bufs=2))
-        ecp = ctx.enter_context(tc.tile_pool(name="ecp", bufs=3))
+        ecp = ctx.enter_context(tc.tile_pool(name="ecp", bufs=4))
         gxp = ctx.enter_context(tc.tile_pool(name="gxp", bufs=3))
         gvp = ctx.enter_context(tc.tile_pool(name="gvp", bufs=2))
         vcp = ctx.enter_context(tc.tile_pool(name="vcp", bufs=2))
@@ -306,13 +306,14 @@ def tile_pgwcrossattention_pa_kernel(tc, q, k, v_ret, pi_star, Wv, bv, gamma, ou
         for t in range(Z_WHOLE):
             for i in range(4):
                 LG(t, i)
+            if t == 0:
+                for i in range(3):
+                    XT(0, i)
             for i in range(4):
                 Z(t, i)
             MR(t)
         w_group()
         w_quant()
-        for t in range(3):
-            XT(0, t)
 
         K1_PIECES = {4: (0,), 5: (1, 2), 6: (3, 4)}
 
@@ -365,7 +366,7 @@ def tile_pgwcrossattention_pa_kernel(tc, q, k, v_ret, pi_star, Wv, bv, gamma, ou
         for i in range(4):
             LG(Z_EARLY, i)
         EX(0)
-        for r in range(N_TILES + 2):
+        for r in range(N_TILES + 3):
             t = Z_EARLY + r
             if r + 1 < N_TILES:
                 EX(r + 1)
@@ -375,8 +376,8 @@ def tile_pgwcrossattention_pa_kernel(tc, q, k, v_ret, pi_star, Wv, bv, gamma, ou
                 EV(r, 0, "s")
                 if r < EV_SHARED:
                     EV(r, 1, "s")
-            if 0 <= r - 2:
-                OM(r - 2)
+            if 0 <= r - 3:
+                OM(r - 3)
             if t < N_TILES:
                 for i in range(4):
                     Z(t, i)
@@ -389,5 +390,5 @@ def tile_pgwcrossattention_pa_kernel(tc, q, k, v_ret, pi_star, Wv, bv, gamma, ou
             if t + 1 < N_TILES:
                 for i in range(4):
                     LG(t + 1, i)
-            if 1 <= r <= N_TILES:
-                M2(r - 1)
+            if 2 <= r <= N_TILES + 1:
+                M2(r - 2)

@@ -24,6 +24,7 @@ LN_AHEAD = 4
 Z_WHOLE = 2
 Z_EARLY = 4
 EV_SHARED = 4
+OM_SHARED = 4
 
 
 def mark(label):
@@ -228,10 +229,14 @@ def tile_pgwcrossattention_pa_kernel(tc, q, k, v_ret, pi_star, Wv, bv, gamma, ou
                                     start=(g == 0), stop=(g == 3))
 
         def OM(t):
-            mark("OM.%d.v" % t)
+            eng = "v" if t < OM_SHARED else "s"
+            mark("OM.%d.%s" % (t, eng))
             b, qt = divmod(t, 4)
             o = op.tile([P, H], F32, name="o")
-            nc.vector.tensor_scalar_mul(out=o[:], in0=S["po", t][:], scalar1=S["ri", t][:, 0:1])
+            if eng == "v":
+                nc.vector.tensor_scalar_mul(out=o[:], in0=S["po", t][:], scalar1=S["ri", t][:, 0:1])
+            else:
+                nc.scalar.activation(out=o[:], in_=S["po", t][:], func=ACT.Copy, scale=S["ri", t][:, 0:1])
             mark("OS.%d" % t)
             nc.sync.dma_start(out=out[b, qt * P:(qt + 1) * P, :], in_=o[:])
 
@@ -315,7 +320,7 @@ def tile_pgwcrossattention_pa_kernel(tc, q, k, v_ret, pi_star, Wv, bv, gamma, ou
         w_group()
         w_quant()
 
-        K1_PIECES = {4: (0,), 5: (1, 2), 6: (3, 4)}
+        K1_PIECES = {5: (0,), 6: (1, 2), 7: (3, 4)}
 
         def z_step(a):
             return divmod(a - 1, 3) if 1 <= a <= 6 else (0, 3)

@@ -56,9 +56,7 @@ def tile_pgwcrossattention_pa_kernel(tc, q, k, v_ret, pi_star, Wv, bv, gamma, ou
         def consts():
             mark("const")
             S["idf"] = const.tile([P, P], F32, name="idf")
-            S["idb"] = const.tile([P, P], BF16, name="idb")
             make_identity(nc, S["idf"][:])
-            make_identity(nc, S["idb"][:])
             S["gam_b"] = const.tile([P, 1], BF16, name="gam_b")
             S["gam"] = const.tile([P, 1], F32, name="gam")
             S["bias"] = const.tile([P, H], BF16, name="bias")
@@ -100,8 +98,8 @@ def tile_pgwcrossattention_pa_kernel(tc, q, k, v_ret, pi_star, Wv, bv, gamma, ou
             mark("LX.%d" % c)
             b, g = divmod(c, 4)
             xr = xrp.tile([P, 4 * DIN], BF16, name="xr")
-            nc.sync.dma_start(out=xr[:].rearrange("p (t d) -> p t d", t=4),
-                              in_=v_ret[b, g * 512:(g + 1) * 512, :].rearrange("(t p) d -> p t d", p=P))
+            nc.sync.dma_start(out=xr[:].rearrange("p (u e d) -> p u e d", u=2, e=2),
+                              in_=v_ret[b, g * 512:(g + 1) * 512, :].rearrange("(u p e) d -> p u e d", u=2, e=2))
             S["xr", c] = xr
 
         def w_group():
@@ -190,18 +188,19 @@ def tile_pgwcrossattention_pa_kernel(tc, q, k, v_ret, pi_star, Wv, bv, gamma, ou
 
         def ET(t, h):
             mark("ET.%d.%d" % (t, h))
-            pe = ps_tp.tile([P, 1024], BF16, name="tp")
+            pe = ps_tp.tile([P, 512], F32, name="tp")
             S["pe", t, h] = pe
-            for j in range(8):
-                jj = h * 8 + j
-                nc.tensor.transpose(pe[:, j * P:(j + 1) * P], S["e", t][:, jj * P:(jj + 1) * P], S["idb"][:])
+            src = S["e", t][:].bitcast(F32)
+            for j in range(4):
+                jj = h * 4 + j
+                nc.tensor.transpose(pe[:, j * P:(j + 1) * P], src[:, jj * P:(jj + 1) * P], S["idf"][:])
 
         def EV(t, h, eng):
             mark("EV.%d.%d.%s" % (t, h, eng))
             if h == 0:
                 S["ge", t] = ep.tile([P, 2048], BF16, name="ge", align_bytes=64)
-            dst = S["ge", t][:, h * 1024:(h + 1) * 1024].rearrange("p (g q t) -> p g q t", g=2, t=4)
-            src = S["pe", t, h][:].rearrange("p (g t q) -> p g q t", g=2, t=4)
+            dst = S["ge", t][:].bitcast(F32)[:, h * 512:(h + 1) * 512].rearrange("p (g q u) -> p g q u", g=2, u=2)
+            src = S["pe", t, h][:].rearrange("p (g u q) -> p g q u", g=2, u=2)
             if eng == "v":
                 nc.vector.tensor_copy(out=dst, in_=src)
             else:

@@ -20,11 +20,9 @@ FLOOR = 1e-9
 BIG = 3.4e38
 N_TILES = B * LQ // P
 N_CHUNKS = B * LK // 512
-LN_AHEAD = 4
-Z_WHOLE = 2
-Z_EARLY = 4
-EV_SHARED = 4
-OM_SHARED = 4
+F_ON_V = 2
+PRE = 4
+M2_LAG = 4
 
 
 def mark(label):
@@ -41,11 +39,11 @@ def tile_pgwcrossattention_pa_kernel(tc, q, k, v_ret, pi_star, Wv, bv, gamma, ou
         kqp = ctx.enter_context(tc.tile_pool(name="kqp", bufs=1))
         ktp = ctx.enter_context(tc.tile_pool(name="ktp", bufs=2))
         ep = ctx.enter_context(tc.tile_pool(name="ep", bufs=2))
-        ecp = ctx.enter_context(tc.tile_pool(name="ecp", bufs=4))
+        ecp = ctx.enter_context(tc.tile_pool(name="ecp", bufs=6))
         gxp = ctx.enter_context(tc.tile_pool(name="gxp", bufs=3))
         gvp = ctx.enter_context(tc.tile_pool(name="gvp", bufs=2))
         vcp = ctx.enter_context(tc.tile_pool(name="vcp", bufs=2))
-        op = ctx.enter_context(tc.tile_pool(name="op", bufs=3))
+        op = ctx.enter_context(tc.tile_pool(name="op", bufs=5))
         stp = ctx.enter_context(tc.tile_pool(name="stp", bufs=8))
         ps_acc = ctx.enter_context(tc.psum_pool(name="ps_acc", bufs=5))
         ps_tp = ctx.enter_context(tc.psum_pool(name="ps_tp", bufs=3))
@@ -228,7 +226,7 @@ def tile_pgwcrossattention_pa_kernel(tc, q, k, v_ret, pi_star, Wv, bv, gamma, ou
                                     start=(g == 0), stop=(g == 3))
 
         def OM(t):
-            eng = "v" if t < OM_SHARED else "s"
+            eng = "s"
             mark("OM.%d.%s" % (t, eng))
             b, qt = divmod(t, 4)
             o = op.tile([P, H], F32, name="o")
@@ -293,106 +291,124 @@ def tile_pgwcrossattention_pa_kernel(tc, q, k, v_ret, pi_star, Wv, bv, gamma, ou
             nc.vector.quantize_mx(out=S["vc", b][:, g * H:(g + 1) * H].bitcast(FP8X4), scales=S["vs", b][:, g * H:(g + 1) * H], in_=S["gv", c][:])
 
         consts()
-        for t in range(3):
-            load_pi(t)
+        load_pi(0)
+        load_pi(1)
         load_q(0)
-        load_pi(3)
+        load_pi(2)
         load_k(0)
-        load_x(0)
-        load_w()
-        for t in range(LN_AHEAD):
-            Fl(t, "v")
-        for t in range(LN_AHEAD):
+        load_pi(3)
+        for t in range(N_TILES):
+            if t >= 4:
+                load_pi(t)
+            Fl(t, "v" if t < F_ON_V else "g")
             LN(t)
         for j in range(5):
             KT(0, j)
             KE(0, j, "v")
-        for t in range(Z_WHOLE):
-            for i in range(4):
-                LG(t, i)
-            if t == 0:
-                for i in range(3):
-                    XT(0, i)
-            for i in range(4):
-                Z(t, i)
-            MR(t)
-        w_group()
-        w_quant()
+        load_q(1)
+        load_k(1)
+        load_x(0)
+        load_w()
+        for c in range(1, 4):
+            load_x(c)
+        units = []
+        for t in range(PRE, N_TILES):
+            units += [(t, 0), (t, 1), (t, 2)]
+        done = [0, 0]
 
-        K1_PIECES = {5: (0,), 6: (1, 2), 7: (3, 4)}
+        def lg_half():
+            if done[1] < 2 * (N_TILES - PRE):
+                t, half = PRE + done[1] // 2, done[1] % 2
+                LG(t, 2 * half)
+                LG(t, 2 * half + 1)
+                done[1] += 1
 
-        def z_step(a):
-            return divmod(a - 1, 3) if 1 <= a <= 6 else (0, 3)
+        def unit():
+            if done[0] < len(units):
+                t, k = units[done[0]]
+                done[0] += 1
+                if k < 2:
+                    Z(t, 2 * k)
+                    Z(t, 2 * k + 1)
+                else:
+                    MR(t)
 
-        for a in range(N_CHUNKS + 2):
-            if a < N_CHUNKS:
-                if a + LN_AHEAD < N_TILES:
-                    load_pi(a + LN_AHEAD)
-                    Fl(a + LN_AHEAD, "g")
-                if a + 1 < N_CHUNKS:
-                    if a + 1 == 5:
-                        load_q(1)
-                        load_k(1)
-                    load_x(a + 1)
-                XE(a, 0)
-                XT(a, 3)
-                for t in range(1, 4):
-                    XE(a, t)
-                if a + LN_AHEAD < N_TILES:
-                    LN(a + LN_AHEAD)
-                for j in K1_PIECES.get(a, ()):
-                    KT(1, j)
-                    KE(1, j, "s")
-            if a >= 2:
-                VE(a - 2)
-            zt, step = z_step(a)
-            if step < 2:
-                Z(Z_WHOLE + zt, 2 * step)
-                Z(Z_WHOLE + zt, 2 * step + 1)
-            elif step == 2:
-                MR(Z_WHOLE + zt)
-            if a >= 2:
-                QV(a - 2)
-            if a < N_CHUNKS:
-                QX(a)
-            if 1 <= a <= N_CHUNKS:
-                M1(a - 1, 0)
-            if a + 1 < N_CHUNKS:
-                for t in range(3):
-                    XT(a + 1, t)
-            if 1 <= a <= N_CHUNKS:
-                M1(a - 1, 1)
-            zt, step = z_step(a + 1)
-            if step < 2:
-                LG(Z_WHOLE + zt, 2 * step)
-                LG(Z_WHOLE + zt, 2 * step + 1)
+        def upcoming(n):
+            want = sum(1 for t, k in units[:done[0] + n] if k < 2)
+            while done[1] < want:
+                lg_half()
 
         for i in range(4):
-            LG(Z_EARLY, i)
-        EX(0)
-        for r in range(N_TILES + 3):
-            t = Z_EARLY + r
-            if r + 1 < N_TILES:
-                EX(r + 1)
+            LG(0, i)
+        w_group()
+        for t in range(4):
+            for i in range(0 if t == 0 else 1, 4):
+                Z(t, i)
+            if t < 3:
+                for i in range(4):
+                    LG(t + 1, i)
+                Z(t + 1, 0)
+            if t == 1:
+                for j in (1, 2, 3, 4, 0):
+                    KT(1, j)
+                    if j > 0 and j < 5:
+                        KE(1, j, "v")
+                    else:
+                        KE(1, j, "s")
+            if t == 2:
+                for i in range(3):
+                    XT(0, i)
+                XE(0, 0)
+                XT(0, 3)
+                for i in range(1, 4):
+                    XE(0, i)
+                for i in range(3):
+                    XT(1, i)
+            if t == 3:
+                QX(0)
+            MR(t)
+            if t == 2:
+                w_quant()
+
+        for r in range(N_TILES + 2):
+            if r < N_TILES:
+                EX(r)
+                M1(r, 0)
+                M1(r, 1)
+            if r >= M2_LAG:
+                M2(r - M2_LAG)
+            if r + 1 < N_CHUNKS:
+                XE(r + 1, 0)
+                XT(r + 1, 3)
+                for i in range(1, 4):
+                    XE(r + 1, i)
+                if r + 4 < N_CHUNKS:
+                    load_x(r + 4)
             if r < N_TILES:
                 ET(r, 0)
                 ET(r, 1)
                 EV(r, 0, "s")
-                if r < EV_SHARED:
-                    EV(r, 1, "s")
-            if 0 <= r - 3:
-                OM(r - 3)
-            if t < N_TILES:
-                for i in range(4):
-                    Z(t, i)
-            if 1 <= r <= N_TILES:
+                EV(r, 1, "s")
+                if r == 7:
+                    QE(r - 1)
+                VE(r)
+            if 1 <= r <= N_TILES and r != 7:
                 QE(r - 1)
-            if t < N_TILES:
-                MR(t)
-            if EV_SHARED <= r < N_TILES:
-                EV(r, 1, "v")
-            if t + 1 < N_TILES:
-                for i in range(4):
-                    LG(t + 1, i)
-            if 2 <= r <= N_TILES + 1:
-                M2(r - 2)
+            if r < N_TILES:
+                QV(r)
+            if r + 2 < N_CHUNKS:
+                XT(r + 2, 0)
+            upcoming(2)
+            if r + 1 < N_CHUNKS:
+                QX(r + 1)
+            unit()
+            unit()
+            if r + 2 < N_CHUNKS:
+                XT(r + 2, 1)
+                XT(r + 2, 2)
+            if r >= M2_LAG:
+                OM(r - M2_LAG)
+        for t in range(N_TILES + 2 - M2_LAG, N_TILES):
+            M2(t)
+        for t in range(N_TILES + 2 - M2_LAG, N_TILES):
+            OM(t)

@@ -55,15 +55,22 @@ def tile_pgwcrossattention_pa_kernel(tc, q, k, v_ret, pi_star, Wv, bv, gamma, ou
             mark("const")
             S["idf"] = const.tile([P, P], F32, name="idf")
             make_identity(nc, S["idf"][:])
-            S["gam_b"] = const.tile([P, 1], BF16, name="gam_b")
-            S["gam"] = const.tile([P, 1], F32, name="gam")
-            S["bias"] = const.tile([P, H], BF16, name="bias")
-            nc.scalar.dma_start(out=S["gam_b"][:], in_=gamma.partition_broadcast(P))
-            nc.scalar.dma_start(out=S["bias"][:], in_=bv.partition_broadcast(P))
+            ones = const.tile([P, P], BF16, name="ones")
+            row = const.tile([P, H + 2], BF16, name="row")
+            S["row"] = const.tile([P, H + 2], F32, name="rowf")
+            nc.vector.memset(row[:], 0.0)
+            nc.vector.memset(ones[:], 1.0)
+            nc.scalar.dma_start(out=row[0:1, H:H + 1], in_=gamma.unsqueeze(0))
+            nc.scalar.dma_start(out=row[0:1, 0:H], in_=bv.unsqueeze(0))
             warm = const.tile([P, 1], F32, name="warm")
             nc.vector.memset(warm[:], 1.0)
             nc.scalar.activation(out=warm[:], in_=warm[:], func=ACT.Ln)
-            nc.vector.tensor_copy(out=S["gam"][:], in_=S["gam_b"][:])
+            pr = ps_acc.tile([P, H + 2], F32, name="acc")
+            nc.tensor.matmul(pr[:], lhsT=ones[:], rhs=row[:], start=True, stop=True)
+            S["pr"] = pr
+
+        def row_copy():
+            nc.vector.tensor_copy(out=S["row"][:], in_=S["pr"][:])
 
         def load_pi(t):
             mark("LP.%d" % t)
@@ -169,7 +176,7 @@ def tile_pgwcrossattention_pa_kernel(tc, q, k, v_ret, pi_star, Wv, bv, gamma, ou
         def Z(t, i):
             mark("Z.%d.%d" % (t, i))
             sl = S["lz", t][:, i * 512:(i + 1) * 512]
-            nc.vector.scalar_tensor_tensor(out=sl, in0=sl, scalar=S["gam"][:, 0:1], in1=S["lg", t, i][:], op0=ALU.mult, op1=ALU.add)
+            nc.vector.scalar_tensor_tensor(out=sl, in0=sl, scalar=S["row"][:, H:H + 1], in1=S["lg", t, i][:], op0=ALU.mult, op1=ALU.add)
 
         def MR(t):
             mark("MR.%d" % t)
@@ -280,7 +287,7 @@ def tile_pgwcrossattention_pa_kernel(tc, q, k, v_ret, pi_star, Wv, bv, gamma, ou
                 mark("VE.%d.%d" % (c, hh))
                 nc.vector.tensor_tensor(out=gv[:, hh * 512:(hh + 1) * 512].rearrange("p (h t) -> p h t", t=4),
                                         in0=S["pv", c, hh][:].rearrange("p (t h) -> p h t", t=4),
-                                        in1=S["bias"][:, hh * P:(hh + 1) * P].unsqueeze(2).to_broadcast([P, P, 4]), op=ALU.add)
+                                        in1=S["row"][:, hh * P:(hh + 1) * P].unsqueeze(2).to_broadcast([P, P, 4]), op=ALU.add)
 
         def QV(c):
             mark("QV.%d" % c)
@@ -302,6 +309,7 @@ def tile_pgwcrossattention_pa_kernel(tc, q, k, v_ret, pi_star, Wv, bv, gamma, ou
                 load_pi(t)
             Fl(t, "v" if t < F_ON_V else "g")
             LN(t)
+        row_copy()
         for j in range(5):
             KT(0, j)
             KE(0, j, "v")

@@ -1,3 +1,4 @@
+import math
 from contextlib import ExitStack
 
 import concourse.mybir as mybir
@@ -16,11 +17,10 @@ AX = mybir.AxisListType
 
 P = 128
 B, LQ, LK, DIN, H = 2, 512, 2048, 1024, 256
-FLOOR = 1e-9
+LOG_FLOOR = math.log(1e-9)
 BIG = 3.4e38
 N_TILES = B * LQ // P
 N_CHUNKS = B * LK // 512
-F_ON_V = 2
 PRE = 4
 M2_LAG = 4
 
@@ -45,8 +45,8 @@ def tile_pgwcrossattention_pa_kernel(tc, q, k, v_ret, pi_star, Wv, bv, gamma, ou
         vcp = ctx.enter_context(tc.tile_pool(name="vcp", bufs=2))
         op = ctx.enter_context(tc.tile_pool(name="op", bufs=5))
         stp = ctx.enter_context(tc.tile_pool(name="stp", bufs=8))
-        ps_acc = ctx.enter_context(tc.psum_pool(name="ps_acc", bufs=5))
-        ps_tp = ctx.enter_context(tc.psum_pool(name="ps_tp", bufs=3))
+        ps_acc = ctx.enter_context(tc.psum_pool(name="ps_acc", bufs=4))
+        ps_tp = ctx.enter_context(tc.psum_pool(name="ps_tp", bufs=4))
         ctx.enter_context(tc.manual_schedule())
 
         S = {}
@@ -57,27 +57,32 @@ def tile_pgwcrossattention_pa_kernel(tc, q, k, v_ret, pi_star, Wv, bv, gamma, ou
             make_identity(nc, S["idf"][:])
             ones = const.tile([P, P], BF16, name="ones")
             row = const.tile([P, H + 2], BF16, name="row")
-            S["row"] = const.tile([P, H + 2], F32, name="rowf")
             nc.vector.memset(row[:], 0.0)
             nc.vector.memset(ones[:], 1.0)
+            S["ones"], S["row_b"] = ones, row
             nc.scalar.dma_start(out=row[0:1, H:H + 1], in_=gamma.unsqueeze(0))
             nc.scalar.dma_start(out=row[0:1, 0:H], in_=bv.unsqueeze(0))
             warm = const.tile([P, 1], F32, name="warm")
             nc.vector.memset(warm[:], 1.0)
+            S["tiny"] = const.tile([P, 1], F32, name="tiny")
+            nc.vector.memset(S["tiny"][:], 2.0 ** -100)
             nc.scalar.activation(out=warm[:], in_=warm[:], func=ACT.Ln)
+
+        def spread_row():
+            mark("ROW")
+            S["row"] = const.tile([P, H + 2], F32, name="rowf")
             pr = ps_acc.tile([P, H + 2], F32, name="acc")
-            nc.tensor.matmul(pr[:], lhsT=ones[:], rhs=row[:], start=True, stop=True)
-            S["pr"] = pr
+            nc.tensor.matmul(pr[:], lhsT=S["ones"][:], rhs=S["row_b"][:], start=True, stop=True)
+            nc.vector.tensor_copy(out=S["row"][:], in_=pr[:])
 
-        def row_copy():
-            nc.vector.tensor_copy(out=S["row"][:], in_=S["pr"][:])
-
-        def load_pi(t):
+        def load_pi(t, pieces=1):
             mark("LP.%d" % t)
             b, qt = divmod(t, 4)
-            x = pip.tile([P, LK], BF16, name="pi")
-            nc.sync.dma_start(out=x[:], in_=pi_star[b, qt * P:(qt + 1) * P, :])
-            S["pi", t] = x
+            x = S["pi", t] = pip.tile([P, LK], BF16, name="pi")
+            w = LK // pieces
+            def piece(i):
+                nc.sync.dma_start(out=x[:, i * w:(i + 1) * w], in_=pi_star[b, qt * P:(qt + 1) * P, i * w:(i + 1) * w])
+            return piece
 
         def load_q(b):
             mark("LQ.%d" % b)
@@ -85,13 +90,13 @@ def tile_pgwcrossattention_pa_kernel(tc, q, k, v_ret, pi_star, Wv, bv, gamma, ou
             nc.sync.dma_start(out=qr[:].rearrange("p (t h) -> p t h", h=H), in_=q[b].rearrange("(t p) h -> p t h", p=P))
             S["qr", b] = qr
 
-        def load_k(b):
-            kr = kqp.tile([P, 16 * H], BF16, name="kr")
-            S["kr", b] = kr
-            for j in range(4):
-                mark("LK.%d.%d" % (b, j))
-                nc.sync.dma_start(out=kr[:, j * 4 * H:(j + 1) * 4 * H].rearrange("p (t h) -> p t h", h=H),
-                                  in_=k[b, j * 512:(j + 1) * 512, :].rearrange("(t p) h -> p t h", p=P))
+        def load_k(b, j):
+            if j == 0:
+                S["kr", b] = kqp.tile([P, 16 * H], BF16, name="kr")
+            kr = S["kr", b]
+            mark("LK.%d.%d" % (b, j))
+            nc.sync.dma_start(out=kr[:, j * 4 * H:(j + 1) * 4 * H].rearrange("p (t h) -> p t h", h=H),
+                              in_=k[b, j * 512:(j + 1) * 512, :].rearrange("(t p) h -> p t h", p=P))
 
         def load_w():
             mark("LW")
@@ -131,46 +136,46 @@ def tile_pgwcrossattention_pa_kernel(tc, q, k, v_ret, pi_star, Wv, bv, gamma, ou
 
         def KE(b, j, eng):
             mark("KE.%d.%d.%s" % (b, j, eng))
-            ps = S["pk", b, j]
             if j == 0:
-                qT = ktp.tile([P, 2, LQ], BF16, name="qT")
-                S["qT", b] = qT
-                src2 = ps[:].bitcast(BF16).rearrange("p (q e) -> p e q", e=2)
+                qT = S["qT", b] = ktp.tile([P, 2 * LQ], BF16, name="qT")
+                src = S["pk", b, j][:].bitcast(BF16)
                 if eng == "v":
-                    nc.vector.tensor_scalar_mul(out=qT[:], in0=src2, scalar1=0.0625)
+                    nc.vector.tensor_scalar_mul(out=qT[:], in0=src, scalar1=0.0625)
                 else:
-                    nc.scalar.activation(out=qT[:], in_=src2, func=ACT.Copy, scale=0.0625)
-            else:
-                if j == 1:
-                    S["kT", b] = ktp.tile([P, 2 * LK], BF16, name="kT")
-                dst = S["kT", b][:].bitcast(F32)[:, (j - 1) * 512:j * 512]
-                if eng == "v":
-                    nc.vector.tensor_copy(out=dst, in_=ps[:])
-                else:
-                    nc.scalar.copy(out=dst, in_=ps[:])
-
-        def Fl(t, eng):
-            mark("F.%d.%s" % (t, eng))
-            x = lzp.tile([P, LK], F32, name="lz")
-            S["lz", t] = x
+                    nc.scalar.activation(out=qT[:], in_=src, func=ACT.Copy, scale=0.0625)
+                return
+            if j == 1:
+                S["kT", b] = ktp.tile([P, 2 * LK], BF16, name="kT")
+            dst = S["kT", b][:].bitcast(F32)[:, (j - 1) * 512:j * 512]
             if eng == "v":
-                nc.vector.tensor_scalar_max(out=x[:], in0=S["pi", t][:], scalar1=FLOOR)
+                nc.vector.tensor_copy(out=dst, in_=S["pk", b, j][:])
             else:
-                nc.gpsimd.tensor_scalar(out=x[:], in0=S["pi", t][:], scalar1=BIG, scalar2=FLOOR, op0=ALU.min, op1=ALU.max)
+                nc.scalar.copy(out=dst, in_=S["pk", b, j][:])
 
-        def LN(t):
+        def LN(t, i=0, n=1):
             mark("LN.%d" % t)
-            x = S["lz", t]
-            nc.scalar.activation(out=x[:], in_=x[:], func=ACT.Ln)
+            if i == 0:
+                S["lz", t] = lzp.tile([P, LK], F32, name="lz")
+            w = slice(i * LK // n, (i + 1) * LK // n)
+            nc.scalar.activation(out=S["lz", t][:, w], in_=S["pi", t][:, w], func=ACT.Ln, bias=S["tiny"][:, 0:1], scale=1.0)
+
+        def Fl(t, i=0, n=1, eng="g"):
+            mark("F.%d" % t)
+            x = S["lz", t][:, i * LK // n:(i + 1) * LK // n]
+            if eng == "v":
+                nc.vector.tensor_scalar_max(out=x, in0=x, scalar1=LOG_FLOOR)
+            else:
+                nc.gpsimd.tensor_scalar(out=x, in0=x, scalar1=BIG, scalar2=LOG_FLOOR, op0=ALU.min, op1=ALU.max)
 
         def LG(t, i):
             mark("LG.%d.%d" % (t, i))
             b, qt = divmod(t, 4)
             lg = ps_acc.tile([P, 512], F32, name="acc")
             S["lg", t, i] = lg
+            qv = S["qT", b][:].rearrange("p (q e) -> p q e", e=2)
             kv = S["kT", b][:].rearrange("p (k e) -> p k e", e=2)
             for e in range(2):
-                nc.tensor.matmul(lg[:], lhsT=S["qT", b][:, e, qt * P:(qt + 1) * P], rhs=kv[:, i * 512:(i + 1) * 512, e],
+                nc.tensor.matmul(lg[:], lhsT=qv[:, qt * P:(qt + 1) * P, e], rhs=kv[:, i * 512:(i + 1) * 512, e],
                                  start=(e == 0), stop=(e == 1))
 
         def Z(t, i):
@@ -217,23 +222,24 @@ def tile_pgwcrossattention_pa_kernel(tc, q, k, v_ret, pi_star, Wv, bv, gamma, ou
             es = ecp.tile([P, 512], U8, name="es", align_bytes=64)
             S["ec", t], S["es", t] = ec, es
             nc.vector.quantize_mx(out=ec[:].bitcast(FP8X4), scales=es[:], in_=S["ge", t][:])
+
+        def OR(t):
             mark("OR.%d" % t)
             ri = stp.tile([P, 1], F32, name="ri")
             S["ri", t] = ri
             nc.vector.reciprocal(out=ri[:], in_=S["rs", t][:])
 
-        def M2(t):
+        def M2(t, gs=range(4)):
             mark("M2.%d" % t)
             b, qt = divmod(t, 4)
-            po = ps_acc.tile([P, H], F32, name="acc")
-            S["po", t] = po
-            for g in range(4):
-                nc.tensor.matmul_mx(po[:], lhsT=S["ec", t][:, g * P:(g + 1) * P].bitcast(FP8X4), lhsT_scale=S["es", t][:, g * P:(g + 1) * P],
+            for g in gs:
+                if g == 0:
+                    S["po", t] = ps_acc.tile([P, H], F32, name="acc")
+                nc.tensor.matmul_mx(S["po", t][:], lhsT=S["ec", t][:, g * P:(g + 1) * P].bitcast(FP8X4), lhsT_scale=S["es", t][:, g * P:(g + 1) * P],
                                     rhs=S["vc", b][:, g * H:(g + 1) * H].bitcast(FP8X4), rhs_scale=S["vs", b][:, g * H:(g + 1) * H],
                                     start=(g == 0), stop=(g == 3))
 
-        def OM(t):
-            eng = "s"
+        def OM(t, eng="s"):
             mark("OM.%d.%s" % (t, eng))
             b, qt = divmod(t, 4)
             o = op.tile([P, H], F32, name="o")
@@ -298,38 +304,54 @@ def tile_pgwcrossattention_pa_kernel(tc, q, k, v_ret, pi_star, Wv, bv, gamma, ou
             nc.vector.quantize_mx(out=S["vc", b][:, g * H:(g + 1) * H].bitcast(FP8X4), scales=S["vs", b][:, g * H:(g + 1) * H], in_=S["gv", c][:])
 
         consts()
-        load_pi(0)
-        load_pi(1)
+        first = load_pi(0, 2)
+        first(0)
         load_q(0)
-        load_pi(2)
-        load_k(0)
-        load_pi(3)
-        for t in range(N_TILES):
-            if t >= 4:
-                load_pi(t)
-            Fl(t, "v" if t < F_ON_V else "g")
-            LN(t)
-        row_copy()
-        for j in range(5):
+        first(1)
+        load_k(0, 0)
+        load_k(0, 1)
+        load_pi(1)(0)
+        load_k(0, 2)
+        load_k(0, 3)
+        load_pi(2)(0)
+        load_pi(3)(0)
+        for i in range(2):
+            LN(0, i, 2)
+            Fl(0, i, 2)
+        for j in range(3):
             KT(0, j)
             KE(0, j, "v")
-        load_q(1)
-        load_k(1)
-        load_x(0)
-        load_w()
-        for c in range(1, 4):
+        spread_row()
+        for i in range(2):
+            LG(0, i)
+        for j in range(3, 5):
+            KT(0, j)
+        for i in range(2):
+            Z(0, i)
+        for j in range(3, 5):
+            KE(0, j, "v")
+        for i in range(2, 4):
+            LG(0, i)
+        for t in range(1, N_TILES):
+            if t >= 4:
+                load_pi(t)(0)
+            LN(t)
+            for i in range(1):
+                Fl(t, i, 1)
+            if t == 3:
+                load_q(1)
+                load_w()
+                w_group()
+            if t == 5:
+                for j in range(4):
+                    load_k(1, j)
+        for c in range(4):
             load_x(c)
+
         units = []
         for t in range(PRE, N_TILES):
             units += [(t, 0), (t, 1), (t, 2)]
         done = [0, 0]
-
-        def lg_half():
-            if done[1] < 2 * (N_TILES - PRE):
-                t, half = PRE + done[1] // 2, done[1] % 2
-                LG(t, 2 * half)
-                LG(t, 2 * half + 1)
-                done[1] += 1
 
         def unit():
             if done[0] < len(units):
@@ -344,79 +366,88 @@ def tile_pgwcrossattention_pa_kernel(tc, q, k, v_ret, pi_star, Wv, bv, gamma, ou
         def upcoming(n):
             want = sum(1 for t, k in units[:done[0] + n] if k < 2)
             while done[1] < want:
-                lg_half()
+                t, half = PRE + done[1] // 2, done[1] % 2
+                LG(t, 2 * half)
+                LG(t, 2 * half + 1)
+                done[1] += 1
 
-        for i in range(4):
-            LG(0, i)
-        w_group()
-        for t in range(4):
-            for i in range(0 if t == 0 else 1, 4):
+        for t in range(PRE):
+            for i in range(2 if t == 0 else 1, 4):
                 Z(t, i)
-            if t < 3:
+            if t + 1 < PRE:
                 for i in range(4):
                     LG(t + 1, i)
                 Z(t + 1, 0)
-            if t == 1:
-                for j in (1, 2, 3, 4, 0):
+            if t == 2:
+                for j in (0, 1, 2, 3, 4):
                     KT(1, j)
-                    if j > 0 and j < 5:
-                        KE(1, j, "v")
-                    else:
-                        KE(1, j, "s")
-            if t == 2:
-                for i in range(3):
-                    XT(0, i)
-                XE(0, 0)
-                XT(0, 3)
-                for i in range(1, 4):
-                    XE(0, i)
-                for i in range(3):
-                    XT(1, i)
-            if t == 3:
-                QX(0)
-            MR(t)
-            if t == 2:
-                w_quant()
+                    KE(1, j, "s" if j in (1, 2, 3, 4,) else "v")
+            if t == PRE - 2:
+                for c in range(2):
+                    for i in range(4):
+                        XT(c, i)
+                    for i in range(4):
+                        XE(c, i)
+                for i in range(2):
+                    XT(2, i)
 
-        for r in range(N_TILES + 2):
-            if r < N_TILES:
-                EX(r)
-                M1(r, 0)
-                M1(r, 1)
-            if r >= M2_LAG:
-                M2(r - M2_LAG)
-            if r + 1 < N_CHUNKS:
-                XE(r + 1, 0)
-                XT(r + 1, 3)
-                for i in range(1, 4):
-                    XE(r + 1, i)
-                if r + 4 < N_CHUNKS:
-                    load_x(r + 4)
-            if r < N_TILES:
-                ET(r, 0)
-                ET(r, 1)
-                EV(r, 0, "s")
-                EV(r, 1, "s")
-                if r == 7:
-                    QE(r - 1)
-                VE(r)
-            if 1 <= r <= N_TILES and r != 7:
-                QE(r - 1)
-            if r < N_TILES:
-                QV(r)
-            if r + 2 < N_CHUNKS:
-                XT(r + 2, 0)
-            upcoming(2)
-            if r + 1 < N_CHUNKS:
+            MR(t)
+        w_quant()
+        load_x(4)
+        upcoming(2)
+        QX(0)
+
+        for r in range(N_TILES):
+            last = r == N_TILES - 1
+            EX(r)
+            if not last:
                 QX(r + 1)
-            unit()
-            unit()
+            for i in range(2):
+                unit()
+            if r >= 1:
+                EV(r - 1, 0, "s" if r - 1 < 8 else "v")
+                EV(r - 1, 1, "s" if r - 1 < 8 else "v")
+            if r >= 6:
+                OM(2 * r - 12, "s")
+                OM(2 * r - 11, "s")
+
             if r + 2 < N_CHUNKS:
-                XT(r + 2, 1)
                 XT(r + 2, 2)
-            if r >= M2_LAG:
-                OM(r - M2_LAG)
-        for t in range(N_TILES + 2 - M2_LAG, N_TILES):
-            M2(t)
-        for t in range(N_TILES + 2 - M2_LAG, N_TILES):
+                XT(r + 2, 3)
+                for i in range(4):
+                    XE(r + 2, i)
+                if r + 5 < N_CHUNKS:
+                    load_x(r + 5)
+            M1(r, 0)
+            M1(r, 1)
+            if 5 <= r < 7:
+                M2(2 * r - 10)
+                M2(2 * r - 9)
+            if last:
+                for t in range(4, 6):
+                    M2(t, range(3))
+            ET(r, 0)
+            ET(r, 1)
+            if last:
+                EV(r, 0, "s")
+            VE(r)
+            if 1 <= r:
+                QE(r - 1)
+                OR(r - 1)
+            QV(r)
+            if last:
+                break
+            if r + 3 < N_CHUNKS:
+                XT(r + 3, 0)
+                XT(r + 3, 1)
+            upcoming(2)
+        EV(7, 1, "v")
+        QE(7)
+        M2(4, range(3, 4))
+        M2(5, range(3, 4))
+        M2(6)
+        for t in (4, 5, 6):
             OM(t)
+        OR(7)
+        M2(7)
+        OM(7)

@@ -81,13 +81,13 @@ def tile_pgwcrossattention_pa_kernel(tc, q, k, v_ret, pi_star, Wv, bv, gamma, ou
             x = S["pi", t] = pip.tile([P, LK], BF16, name="pi")
             w = LK // pieces
             def piece(i):
-                nc.sync.dma_start(out=x[:, i * w:(i + 1) * w], in_=pi_star[b, qt * P:(qt + 1) * P, i * w:(i + 1) * w])
+                nc.sync.dma_start(out=x[:, i * w:(i + 1) * w], in_=pi_star[b].rearrange("(p t) k -> t p k", t=4)[qt, :, i * w:(i + 1) * w])
             return piece
 
         def load_q(b):
             mark("LQ.%d" % b)
             qr = kqp.tile([P, 4 * H], BF16, name="qr")
-            nc.sync.dma_start(out=qr[:].rearrange("p (t h) -> p t h", h=H), in_=q[b].rearrange("(t p) h -> p t h", p=P))
+            nc.sync.dma_start(out=qr[:], in_=q[b].rearrange("(p t) h -> p (t h)", t=4))
             S["qr", b] = qr
 
         def load_k(b, j):
@@ -95,8 +95,7 @@ def tile_pgwcrossattention_pa_kernel(tc, q, k, v_ret, pi_star, Wv, bv, gamma, ou
                 S["kr", b] = kqp.tile([P, 16 * H], BF16, name="kr")
             kr = S["kr", b]
             mark("LK.%d.%d" % (b, j))
-            nc.sync.dma_start(out=kr[:, j * 4 * H:(j + 1) * 4 * H].rearrange("p (t h) -> p t h", h=H),
-                              in_=k[b, j * 512:(j + 1) * 512, :].rearrange("(t p) h -> p t h", p=P))
+            nc.sync.dma_start(out=kr[:, j * 4 * H:(j + 1) * 4 * H], in_=k[b, j * 512:(j + 1) * 512, :].rearrange("(p t) h -> p (t h)", t=4))
 
         def load_w():
             mark("LW")
@@ -146,11 +145,12 @@ def tile_pgwcrossattention_pa_kernel(tc, q, k, v_ret, pi_star, Wv, bv, gamma, ou
                 return
             if j == 1:
                 S["kT", b] = ktp.tile([P, 2 * LK], BF16, name="kT")
-            dst = S["kT", b][:].bitcast(F32)[:, (j - 1) * 512:j * 512]
+            dst = S["kT", b][:].bitcast(F32)[:, (j - 1) * 512:j * 512].rearrange("p (k t) -> p k t", t=4)
+            src = S["pk", b, j][:].rearrange("p (t k) -> p k t", t=4)
             if eng == "v":
-                nc.vector.tensor_copy(out=dst, in_=S["pk", b, j][:])
+                nc.vector.tensor_copy(out=dst, in_=src)
             else:
-                nc.scalar.copy(out=dst, in_=S["pk", b, j][:])
+                nc.scalar.copy(out=dst, in_=src)
 
         def LN(t, i=0, n=1):
             mark("LN.%d" % t)
@@ -196,6 +196,20 @@ def tile_pgwcrossattention_pa_kernel(tc, q, k, v_ret, pi_star, Wv, bv, gamma, ou
             S["e", t], S["rs", t] = e, rs
             nc.scalar.activation(out=e[:], in_=S["lz", t][:], func=ACT.Exp, bias=S["nm", t][:, 0:1], scale=1.0, accum_out=rs[:, 0:1])
 
+        def EX_half(t, h):
+            mark("EX.%d.%d" % (t, h))
+            if h == 0:
+                S["e", t] = ep.tile([P, LK], BF16, name="e")
+                S["rs2", t] = stp.tile([P, 2], F32, name="rs2")
+            w = slice(h * LK // 2, (h + 1) * LK // 2)
+            nc.scalar.activation(out=S["e", t][:, w], in_=S["lz", t][:, w], func=ACT.Exp, bias=S["nm", t][:, 0:1], scale=1.0,
+                                 accum_out=S["rs2", t][:, h:h + 1])
+
+        def RS(t):
+            mark("RS.%d" % t)
+            rs = S["rs", t] = stp.tile([P, 1], F32, name="rs")
+            nc.vector.tensor_tensor(out=rs[:], in0=S["rs2", t][:, 0:1], in1=S["rs2", t][:, 1:2], op=ALU.add)
+
         def ET(t, h):
             mark("ET.%d.%d" % (t, h))
             pe = ps_tp.tile([P, 512], F32, name="tp")
@@ -223,6 +237,14 @@ def tile_pgwcrossattention_pa_kernel(tc, q, k, v_ret, pi_star, Wv, bv, gamma, ou
             S["ec", t], S["es", t] = ec, es
             nc.vector.quantize_mx(out=ec[:].bitcast(FP8X4), scales=es[:], in_=S["ge", t][:])
 
+        def QE_half(t, h):
+            mark("QE.%d.%d" % (t, h))
+            if h == 0:
+                S["ec", t] = ecp.tile([P, 512], U32, name="ec", align_bytes=64)
+                S["es", t] = ecp.tile([P, 512], U8, name="es", align_bytes=64)
+            w = slice(h * 256, (h + 1) * 256)
+            nc.vector.quantize_mx(out=S["ec", t][:, w].bitcast(FP8X4), scales=S["es", t][:, w], in_=S["ge", t][:, h * 1024:(h + 1) * 1024])
+
         def OR(t):
             mark("OR.%d" % t)
             ri = stp.tile([P, 1], F32, name="ri")
@@ -248,7 +270,7 @@ def tile_pgwcrossattention_pa_kernel(tc, q, k, v_ret, pi_star, Wv, bv, gamma, ou
             else:
                 nc.scalar.activation(out=o[:], in_=S["po", t][:], func=ACT.Copy, scale=S["ri", t][:, 0:1])
             mark("OS.%d" % t)
-            nc.sync.dma_start(out=out[b, qt * P:(qt + 1) * P, :], in_=o[:])
+            nc.sync.dma_start(out=out[b].rearrange("(p t) h -> t p h", t=4)[qt], in_=o[:])
 
         def XT(c, t):
             mark("XT.%d.%d" % (c, t))
@@ -399,11 +421,17 @@ def tile_pgwcrossattention_pa_kernel(tc, q, k, v_ret, pi_star, Wv, bv, gamma, ou
 
         for r in range(N_TILES):
             last = r == N_TILES - 1
-            EX(r)
             if not last:
+                EX(r)
+            if not last and r >= 2:
                 QX(r + 1)
             for i in range(2):
                 unit()
+            if r < 2:
+                QX(r + 1)
+            if last:
+                EX_half(r, 0)
+                EX_half(r, 1)
             if r >= 1:
                 EV(r - 1, 0, "s" if r - 1 < 8 else "v")
                 EV(r - 1, 1, "s" if r - 1 < 8 else "v")
@@ -418,6 +446,10 @@ def tile_pgwcrossattention_pa_kernel(tc, q, k, v_ret, pi_star, Wv, bv, gamma, ou
                     XE(r + 2, i)
                 if r + 5 < N_CHUNKS:
                     load_x(r + 5)
+            if r >= 6:
+                ET(r, 0)
+                if not last:
+                    ET(r, 1)
             M1(r, 0)
             M1(r, 1)
             if 5 <= r < 7:
@@ -426,10 +458,11 @@ def tile_pgwcrossattention_pa_kernel(tc, q, k, v_ret, pi_star, Wv, bv, gamma, ou
             if last:
                 for t in range(4, 6):
                     M2(t, range(3))
-            ET(r, 0)
-            ET(r, 1)
+            if r < 6:
+                ET(r, 0)
+                ET(r, 1)
             if last:
-                EV(r, 0, "s")
+                ET(r, 1)
             VE(r)
             if 1 <= r:
                 QE(r - 1)
@@ -441,13 +474,16 @@ def tile_pgwcrossattention_pa_kernel(tc, q, k, v_ret, pi_star, Wv, bv, gamma, ou
                 XT(r + 3, 0)
                 XT(r + 3, 1)
             upcoming(2)
-        EV(7, 1, "v")
-        QE(7)
+        RS(7)
+        EV(7, 0, "s")
+        OR(7)
         M2(4, range(3, 4))
         M2(5, range(3, 4))
         M2(6)
+        QE_half(7, 0)
+        EV(7, 1, "s")
+        QE_half(7, 1)
         for t in (4, 5, 6):
             OM(t)
-        OR(7)
         M2(7)
         OM(7)

@@ -326,26 +326,32 @@ def tile_pgwcrossattention_pa_kernel(tc, q, k, v_ret, pi_star, Wv, bv, gamma, ou
             nc.vector.quantize_mx(out=S["vc", b][:, g * H:(g + 1) * H].bitcast(FP8X4), scales=S["vs", b][:, g * H:(g + 1) * H], in_=S["gv", c][:])
 
         consts()
-        first = load_pi(0, 2)
-        first(0)
+        plan0 = load_pi(0, 2)
+        plan1 = load_pi(1, 2)
+        plan0(0)
         load_q(0)
-        first(1)
         load_k(0, 0)
         load_k(0, 1)
-        load_pi(1)(0)
+        plan0(1)
+        plan1(0)
         load_k(0, 2)
         load_k(0, 3)
+        plan1(1)
         load_pi(2)(0)
         load_pi(3)(0)
-        for i in range(2):
-            LN(0, i, 2)
-            Fl(0, i, 2)
-        for j in range(3):
+        for t in range(2):
+            for i in range(2):
+                LN(t, i, 2)
+                Fl(t, i, 2)
+        KT(0, 0)
+        KE(0, 0, "v")
+        for j in range(1, 3):
             KT(0, j)
             KE(0, j, "v")
         spread_row()
         for i in range(2):
             LG(0, i)
+
         for j in range(3, 5):
             KT(0, j)
         for i in range(2):
@@ -354,7 +360,7 @@ def tile_pgwcrossattention_pa_kernel(tc, q, k, v_ret, pi_star, Wv, bv, gamma, ou
             KE(0, j, "v")
         for i in range(2, 4):
             LG(0, i)
-        for t in range(1, N_TILES):
+        for t in range(2, N_TILES):
             if t >= 4:
                 load_pi(t)(0)
             LN(t)
@@ -400,6 +406,7 @@ def tile_pgwcrossattention_pa_kernel(tc, q, k, v_ret, pi_star, Wv, bv, gamma, ou
                 for i in range(4):
                     LG(t + 1, i)
                 Z(t + 1, 0)
+            MR(t)
             if t == 2:
                 for j in (0, 1, 2, 3, 4):
                     KT(1, j)
@@ -413,7 +420,6 @@ def tile_pgwcrossattention_pa_kernel(tc, q, k, v_ret, pi_star, Wv, bv, gamma, ou
                 for i in range(2):
                     XT(2, i)
 
-            MR(t)
         w_quant()
         load_x(4)
         upcoming(2)
@@ -425,8 +431,10 @@ def tile_pgwcrossattention_pa_kernel(tc, q, k, v_ret, pi_star, Wv, bv, gamma, ou
                 EX(r)
             if not last and r >= 2:
                 QX(r + 1)
-            for i in range(2):
-                unit()
+            unit()
+            if r >= 1:
+                QV(r - 1)
+            unit()
             if r < 2:
                 QX(r + 1)
             if last:
@@ -439,6 +447,9 @@ def tile_pgwcrossattention_pa_kernel(tc, q, k, v_ret, pi_star, Wv, bv, gamma, ou
                 OM(2 * r - 12, "s")
                 OM(2 * r - 11, "s")
 
+            if r < 2:
+                M1(r, 0)
+                M1(r, 1)
             if r + 2 < N_CHUNKS:
                 XT(r + 2, 2)
                 XT(r + 2, 3)
@@ -450,8 +461,9 @@ def tile_pgwcrossattention_pa_kernel(tc, q, k, v_ret, pi_star, Wv, bv, gamma, ou
                 ET(r, 0)
                 if not last:
                     ET(r, 1)
-            M1(r, 0)
-            M1(r, 1)
+            if r >= 2:
+                M1(r, 0)
+                M1(r, 1)
             if 5 <= r < 7:
                 M2(2 * r - 10)
                 M2(2 * r - 9)
@@ -467,7 +479,8 @@ def tile_pgwcrossattention_pa_kernel(tc, q, k, v_ret, pi_star, Wv, bv, gamma, ou
             if 1 <= r:
                 QE(r - 1)
                 OR(r - 1)
-            QV(r)
+            if last:
+                QV(r)
             if last:
                 break
             if r + 3 < N_CHUNKS:

@@ -192,9 +192,11 @@ def tile_pgwcrossattention_pa_kernel(tc, q, k, v_ret, pi_star, Wv, bv, gamma, ou
         def EX(t):
             mark("EX.%d" % t)
             e = ep.tile([P, LK], BF16, name="e")
-            rs = stp.tile([P, 1], F32, name="rs")
-            S["e", t], S["rs", t] = e, rs
-            nc.scalar.activation(out=e[:], in_=S["lz", t][:], func=ACT.Exp, bias=S["nm", t][:, 0:1], scale=1.0, accum_out=rs[:, 0:1])
+            b, qt = divmod(t, 4)
+            if qt == 0:
+                S["rs", b] = const.tile([P, 4], F32, name="rs%d" % b)
+            S["e", t] = e
+            nc.scalar.activation(out=e[:], in_=S["lz", t][:], func=ACT.Exp, bias=S["nm", t][:, 0:1], scale=1.0, accum_out=S["rs", b][:, qt:qt + 1])
 
         def EX_half(t, h):
             mark("EX.%d.%d" % (t, h))
@@ -207,8 +209,7 @@ def tile_pgwcrossattention_pa_kernel(tc, q, k, v_ret, pi_star, Wv, bv, gamma, ou
 
         def RS(t):
             mark("RS.%d" % t)
-            rs = S["rs", t] = stp.tile([P, 1], F32, name="rs")
-            nc.vector.tensor_tensor(out=rs[:], in0=S["rs2", t][:, 0:1], in1=S["rs2", t][:, 1:2], op=ALU.add)
+            nc.vector.tensor_tensor(out=S["rs", 1][:, 3:4], in0=S["rs2", t][:, 0:1], in1=S["rs2", t][:, 1:2], op=ALU.add)
 
         def ET(t, h):
             mark("ET.%d.%d" % (t, h))
@@ -245,11 +246,10 @@ def tile_pgwcrossattention_pa_kernel(tc, q, k, v_ret, pi_star, Wv, bv, gamma, ou
             w = slice(h * 256, (h + 1) * 256)
             nc.vector.quantize_mx(out=S["ec", t][:, w].bitcast(FP8X4), scales=S["es", t][:, w], in_=S["ge", t][:, h * 1024:(h + 1) * 1024])
 
-        def OR(t):
-            mark("OR.%d" % t)
-            ri = stp.tile([P, 1], F32, name="ri")
-            S["ri", t] = ri
-            nc.vector.reciprocal(out=ri[:], in_=S["rs", t][:])
+        def OR(b):
+            mark("OR.%d" % b)
+            S["ri", b] = const.tile([P, 4], F32, name="ri%d" % b)
+            nc.vector.reciprocal(out=S["ri", b][:], in_=S["rs", b][:])
 
         def M2(t, gs=range(4)):
             mark("M2.%d" % t)
@@ -266,9 +266,9 @@ def tile_pgwcrossattention_pa_kernel(tc, q, k, v_ret, pi_star, Wv, bv, gamma, ou
             b, qt = divmod(t, 4)
             o = op.tile([P, H], F32, name="o")
             if eng == "v":
-                nc.vector.tensor_scalar_mul(out=o[:], in0=S["po", t][:], scalar1=S["ri", t][:, 0:1])
+                nc.vector.tensor_scalar_mul(out=o[:], in0=S["po", t][:], scalar1=S["ri", b][:, qt:qt + 1])
             else:
-                nc.scalar.activation(out=o[:], in_=S["po", t][:], func=ACT.Copy, scale=S["ri", t][:, 0:1])
+                nc.scalar.activation(out=o[:], in_=S["po", t][:], func=ACT.Copy, scale=S["ri", b][:, qt:qt + 1])
             mark("OS.%d" % t)
             nc.sync.dma_start(out=out[b].rearrange("(p t) h -> t p h", t=4)[qt], in_=o[:])
 
@@ -356,8 +356,7 @@ def tile_pgwcrossattention_pa_kernel(tc, q, k, v_ret, pi_star, Wv, bv, gamma, ou
             KT(0, j)
         for i in range(2):
             Z(0, i)
-        for j in range(3, 5):
-            KE(0, j, "v")
+            KE(0, i + 3, "v")
         for i in range(2, 4):
             LG(0, i)
         for t in range(2, N_TILES):
@@ -368,11 +367,12 @@ def tile_pgwcrossattention_pa_kernel(tc, q, k, v_ret, pi_star, Wv, bv, gamma, ou
                 Fl(t, i, 1)
             if t == 3:
                 load_q(1)
-                load_w()
-                w_group()
-            if t == 5:
+            if t == 4:
                 for j in range(4):
                     load_k(1, j)
+            if t == 5:
+                load_w()
+                w_group()
         for c in range(4):
             load_x(c)
 
@@ -402,15 +402,19 @@ def tile_pgwcrossattention_pa_kernel(tc, q, k, v_ret, pi_star, Wv, bv, gamma, ou
         for t in range(PRE):
             for i in range(2 if t == 0 else 1, 4):
                 Z(t, i)
+            if t == 2:
+                for j in range(4):
+                    KT(1, j)
             if t + 1 < PRE:
                 for i in range(4):
                     LG(t + 1, i)
                 Z(t + 1, 0)
-            MR(t)
             if t == 2:
-                for j in (0, 1, 2, 3, 4):
-                    KT(1, j)
-                    KE(1, j, "s" if j in (1, 2, 3, 4,) else "v")
+                KE(1, 0, "v")
+                KT(1, 4)
+                for j in range(1, 5):
+                    KE(1, j, "s")
+            MR(t)
             if t == PRE - 2:
                 for c in range(2):
                     for i in range(4):
@@ -467,18 +471,18 @@ def tile_pgwcrossattention_pa_kernel(tc, q, k, v_ret, pi_star, Wv, bv, gamma, ou
             if 5 <= r < 7:
                 M2(2 * r - 10)
                 M2(2 * r - 9)
-            if last:
-                for t in range(4, 6):
-                    M2(t, range(3))
             if r < 6:
                 ET(r, 0)
                 ET(r, 1)
             if last:
                 ET(r, 1)
+                for t in range(4, 6):
+                    M2(t, range(3))
             VE(r)
             if 1 <= r:
                 QE(r - 1)
-                OR(r - 1)
+            if r == 4:
+                OR(0)
             if last:
                 QV(r)
             if last:
@@ -489,7 +493,7 @@ def tile_pgwcrossattention_pa_kernel(tc, q, k, v_ret, pi_star, Wv, bv, gamma, ou
             upcoming(2)
         RS(7)
         EV(7, 0, "s")
-        OR(7)
+        OR(1)
         M2(4, range(3, 4))
         M2(5, range(3, 4))
         M2(6)

@@ -326,40 +326,35 @@ def tile_pgwcrossattention_pa_kernel(tc, q, k, v_ret, pi_star, Wv, bv, gamma, ou
             nc.vector.quantize_mx(out=S["vc", b][:, g * H:(g + 1) * H].bitcast(FP8X4), scales=S["vs", b][:, g * H:(g + 1) * H], in_=S["gv", c][:])
 
         consts()
-        plan0 = load_pi(0, 2)
-        plan1 = load_pi(1, 2)
-        plan0(0)
+        first = load_pi(0, 2)
+        first(0)
         load_q(0)
+        first(1)
         load_k(0, 0)
         load_k(0, 1)
-        plan0(1)
-        plan1(0)
+        load_pi(1)(0)
         load_k(0, 2)
         load_k(0, 3)
-        plan1(1)
         load_pi(2)(0)
         load_pi(3)(0)
-        for t in range(2):
-            for i in range(2):
-                LN(t, i, 2)
-                Fl(t, i, 2)
-        KT(0, 0)
-        KE(0, 0, "v")
-        for j in range(1, 3):
+        for i in range(2):
+            LN(0, i, 2)
+            Fl(0, i, 2)
+        for j in range(3):
             KT(0, j)
             KE(0, j, "v")
         spread_row()
         for i in range(2):
             LG(0, i)
-
         for j in range(3, 5):
             KT(0, j)
         for i in range(2):
             Z(0, i)
-            KE(0, i + 3, "v")
+        for j in range(3, 5):
+            KE(0, j, "v")
         for i in range(2, 4):
             LG(0, i)
-        for t in range(2, N_TILES):
+        for t in range(1, N_TILES):
             if t >= 4:
                 load_pi(t)(0)
             LN(t)

import math
from contextlib import ExitStack

import concourse.mybir as mybir
from concourse.masks import make_identity

FLOPS = 2 * 2 * (2048 * 1024 * 256 + 2 * 512 * 2048 * 256)

BF16 = mybir.dt.bfloat16
F32 = mybir.dt.float32
U32 = mybir.dt.uint32
U8 = mybir.dt.uint8
FP8X4 = mybir.dt.float8_e4m3fn_x4
ALU = mybir.AluOpType
ACT = mybir.ActivationFunctionType
AX = mybir.AxisListType

P = 128
B, LQ, LK, DIN, H = 2, 512, 2048, 1024, 256
LOG_FLOOR = math.log(1e-9)
BIG = 3.4e38
N_TILES = B * LQ // P
N_CHUNKS = B * LK // 512
PRE = 4
M2_LAG = 4


def mark(label):
    return label


def tile_pgwcrossattention_pa_kernel(tc, q, k, v_ret, pi_star, Wv, bv, gamma, out):
    nc = tc.nc
    with ExitStack() as ctx:
        const = ctx.enter_context(tc.tile_pool(name="const", bufs=1))
        pip = ctx.enter_context(tc.tile_pool(name="pip", bufs=4))
        lzp = ctx.enter_context(tc.tile_pool(name="lzp", bufs=8))
        xrp = ctx.enter_context(tc.tile_pool(name="xrp", bufs=4))
        kqp = ctx.enter_context(tc.tile_pool(name="kqp", bufs=1))
        ktp = ctx.enter_context(tc.tile_pool(name="ktp", bufs=2))
        ep = ctx.enter_context(tc.tile_pool(name="ep", bufs=2))
        ecp = ctx.enter_context(tc.tile_pool(name="ecp", bufs=6))
        gxp = ctx.enter_context(tc.tile_pool(name="gxp", bufs=3))
        gvp = ctx.enter_context(tc.tile_pool(name="gvp", bufs=2))
        vcp = ctx.enter_context(tc.tile_pool(name="vcp", bufs=2))
        op = ctx.enter_context(tc.tile_pool(name="op", bufs=5))
        stp = ctx.enter_context(tc.tile_pool(name="stp", bufs=8))
        ps_acc = ctx.enter_context(tc.psum_pool(name="ps_acc", bufs=4))
        ps_tp = ctx.enter_context(tc.psum_pool(name="ps_tp", bufs=4))
        ctx.enter_context(tc.manual_schedule())

        S = {}

        def consts():
            mark("const")
            S["idf"] = const.tile([P, P], F32, name="idf")
            make_identity(nc, S["idf"][:])
            ones = const.tile([P, P], BF16, name="ones")
            row = const.tile([P, H + 2], BF16, name="row")
            nc.vector.memset(row[:], 0.0)
            nc.vector.memset(ones[:], 1.0)
            S["ones"], S["row_b"] = ones, row
            nc.scalar.dma_start(out=row[0:1, H:H + 1], in_=gamma.unsqueeze(0))
            nc.scalar.dma_start(out=row[0:1, 0:H], in_=bv.unsqueeze(0))
            warm = const.tile([P, 1], F32, name="warm")
            nc.vector.memset(warm[:], 1.0)
            S["tiny"] = const.tile([P, 1], F32, name="tiny")
            nc.vector.memset(S["tiny"][:], 2.0 ** -100)
            nc.scalar.activation(out=warm[:], in_=warm[:], func=ACT.Ln)

        def spread_row():
            mark("ROW")
            S["row"] = const.tile([P, H + 2], F32, name="rowf")
            pr = ps_acc.tile([P, H + 2], F32, name="acc")
            nc.tensor.matmul(pr[:], lhsT=S["ones"][:], rhs=S["row_b"][:], start=True, stop=True)
            nc.vector.tensor_copy(out=S["row"][:], in_=pr[:])

        def load_pi(t, pieces=1):
            mark("LP.%d" % t)
            b, qt = divmod(t, 4)
            x = S["pi", t] = pip.tile([P, LK], BF16, name="pi")
            w = LK // pieces
            def piece(i):
                nc.sync.dma_start(out=x[:, i * w:(i + 1) * w], in_=pi_star[b].rearrange("(p t) k -> t p k", t=4)[qt, :, i * w:(i + 1) * w])
            return piece

        def load_q(b):
            mark("LQ.%d" % b)
            qr = kqp.tile([P, 4 * H], BF16, name="qr")
            nc.sync.dma_start(out=qr[:], in_=q[b].rearrange("(p t) h -> p (t h)", t=4))
            S["qr", b] = qr

        def load_k(b, j):
            if j == 0:
                S["kr", b] = kqp.tile([P, 16 * H], BF16, name="kr")
            kr = S["kr", b]
            mark("LK.%d.%d" % (b, j))
            nc.sync.dma_start(out=kr[:, j * 4 * H:(j + 1) * 4 * H], in_=k[b, j * 512:(j + 1) * 512, :].rearrange("(p t) h -> p (t h)", t=4))

        def load_w():
            mark("LW")
            wr = ep.tile([P, 2048], BF16, name="e")
            nc.sync.dma_start(out=wr[:].rearrange("p (c x) -> p c x", c=4), in_=Wv.rearrange("(c p e) h -> p c (e h)", p=P, e=2))
            S["wr"] = wr

        def load_x(c):
            mark("LX.%d" % c)
            b, g = divmod(c, 4)
            xr = xrp.tile([P, 4 * DIN], BF16, name="xr")
            nc.sync.dma_start(out=xr[:].rearrange("p (u e d) -> p u e d", u=2, e=2),
                              in_=v_ret[b, g * 512:(g + 1) * 512, :].rearrange("(u p e) d -> p u e d", u=2, e=2))
            S["xr", c] = xr

        def w_group():
            mark("WG.g")
            wg = ep.tile([P, 2048], BF16, name="ge", align_bytes=64)
            S["wg"] = wg
            nc.gpsimd.tensor_scalar(out=wg[:].rearrange("p (g h t) -> p g h t", g=2, t=4),
                                    in0=S["wr"][:].rearrange("p (g t h) -> p g h t", g=2, t=4), scalar1=1.0, scalar2=0.0, op0=ALU.mult, op1=ALU.add)

        def w_quant():
            mark("WQ")
            wc = const.tile([P, 512], U32, name="wc", align_bytes=64)
            ws = const.tile([P, 512], U8, name="ws", align_bytes=64)
            nc.vector.quantize_mx(out=wc[:].bitcast(FP8X4), scales=ws[:], in_=S["wg"][:])
            S["wc"], S["ws"] = wc, ws

        def KT(b, j):
            mark("KT.%d.%d" % (b, j))
            ps = ps_tp.tile([P, 512], F32, name="tp")
            S["pk", b, j] = ps
            src = S["qr", b][:].bitcast(F32) if j == 0 else S["kr", b][:].bitcast(F32)[:, (j - 1) * 512:j * 512]
            for i in range(4):
                nc.tensor.transpose(ps[:, i * P:(i + 1) * P], src[:, i * P:(i + 1) * P], S["idf"][:])

        def KE(b, j, eng):
            mark("KE.%d.%d.%s" % (b, j, eng))
            if j == 0:
                qT = S["qT", b] = ktp.tile([P, 2 * LQ], BF16, name="qT")
                src = S["pk", b, j][:].bitcast(BF16)
                if eng == "v":
                    nc.vector.tensor_scalar_mul(out=qT[:], in0=src, scalar1=0.0625)
                else:
                    nc.scalar.activation(out=qT[:], in_=src, func=ACT.Copy, scale=0.0625)
                return
            if j == 1:
                S["kT", b] = ktp.tile([P, 2 * LK], BF16, name="kT")
            dst = S["kT", b][:].bitcast(F32)[:, (j - 1) * 512:j * 512].rearrange("p (k t) -> p k t", t=4)
            src = S["pk", b, j][:].rearrange("p (t k) -> p k t", t=4)
            if eng == "v":
                nc.vector.tensor_copy(out=dst, in_=src)
            else:
                nc.scalar.copy(out=dst, in_=src)

        def LN(t, i=0, n=1):
            mark("LN.%d" % t)
            if i == 0:
                S["lz", t] = lzp.tile([P, LK], F32, name="lz")
            w = slice(i * LK // n, (i + 1) * LK // n)
            nc.scalar.activation(out=S["lz", t][:, w], in_=S["pi", t][:, w], func=ACT.Ln, bias=S["tiny"][:, 0:1], scale=1.0)

        def Fl(t, i=0, n=1, eng="g"):
            mark("F.%d" % t)
            x = S["lz", t][:, i * LK // n:(i + 1) * LK // n]
            if eng == "v":
                nc.vector.tensor_scalar_max(out=x, in0=x, scalar1=LOG_FLOOR)
            else:
                nc.gpsimd.tensor_scalar(out=x, in0=x, scalar1=BIG, scalar2=LOG_FLOOR, op0=ALU.min, op1=ALU.max)

        def LG(t, i):
            mark("LG.%d.%d" % (t, i))
            b, qt = divmod(t, 4)
            lg = ps_acc.tile([P, 512], F32, name="acc")
            S["lg", t, i] = lg
            qv = S["qT", b][:].rearrange("p (q e) -> p q e", e=2)
            kv = S["kT", b][:].rearrange("p (k e) -> p k e", e=2)
            for e in range(2):
                nc.tensor.matmul(lg[:], lhsT=qv[:, qt * P:(qt + 1) * P, e], rhs=kv[:, i * 512:(i + 1) * 512, e],
                                 start=(e == 0), stop=(e == 1))

        def Z(t, i):
            mark("Z.%d.%d" % (t, i))
            sl = S["lz", t][:, i * 512:(i + 1) * 512]
            nc.vector.scalar_tensor_tensor(out=sl, in0=sl, scalar=S["row"][:, H:H + 1], in1=S["lg", t, i][:], op0=ALU.mult, op1=ALU.add)

        def MR(t):
            mark("MR.%d" % t)
            nm = stp.tile([P, 1], F32, name="nm")
            S["nm", t] = nm
            nc.vector.tensor_reduce(out=nm[:], in_=S["lz", t][:], axis=AX.X, op=ALU.max, negate=True)

        def EX(t):
            mark("EX.%d" % t)
            e = ep.tile([P, LK], BF16, name="e")
            b, qt = divmod(t, 4)
            if qt == 0:
                S["rs", b] = const.tile([P, 4], F32, name="rs%d" % b)
            S["e", t] = e
            nc.scalar.activation(out=e[:], in_=S["lz", t][:], func=ACT.Exp, bias=S["nm", t][:, 0:1], scale=1.0, accum_out=S["rs", b][:, qt:qt + 1])

        def EX_half(t, h):
            mark("EX.%d.%d" % (t, h))
            if h == 0:
                S["e", t] = ep.tile([P, LK], BF16, name="e")
                S["rs2", t] = stp.tile([P, 2], F32, name="rs2")
            w = slice(h * LK // 2, (h + 1) * LK // 2)
            nc.scalar.activation(out=S["e", t][:, w], in_=S["lz", t][:, w], func=ACT.Exp, bias=S["nm", t][:, 0:1], scale=1.0,
                                 accum_out=S["rs2", t][:, h:h + 1])

        def RS(t):
            mark("RS.%d" % t)
            nc.vector.tensor_tensor(out=S["rs", 1][:, 3:4], in0=S["rs2", t][:, 0:1], in1=S["rs2", t][:, 1:2], op=ALU.add)

        def ET(t, h):
            mark("ET.%d.%d" % (t, h))
            pe = ps_tp.tile([P, 512], F32, name="tp")
            S["pe", t, h] = pe
            src = S["e", t][:].bitcast(F32)
            for j in range(4):
                jj = h * 4 + j
                nc.tensor.transpose(pe[:, j * P:(j + 1) * P], src[:, jj * P:(jj + 1) * P], S["idf"][:])

        def EV(t, h, eng):
            mark("EV.%d.%d.%s" % (t, h, eng))
            if h == 0:
                S["ge", t] = ep.tile([P, 2048], BF16, name="ge", align_bytes=64)
            dst = S["ge", t][:].bitcast(F32)[:, h * 512:(h + 1) * 512].rearrange("p (g q u) -> p g q u", g=2, u=2)
            src = S["pe", t, h][:].rearrange("p (g u q) -> p g q u", g=2, u=2)
            if eng == "v":
                nc.vector.tensor_copy(out=dst, in_=src)
            else:
                nc.scalar.copy(out=dst, in_=src)

        def QE(t):
            mark("QE.%d" % t)
            ec = ecp.tile([P, 512], U32, name="ec", align_bytes=64)
            es = ecp.tile([P, 512], U8, name="es", align_bytes=64)
            S["ec", t], S["es", t] = ec, es
            nc.vector.quantize_mx(out=ec[:].bitcast(FP8X4), scales=es[:], in_=S["ge", t][:])

        def QE_half(t, h):
            mark("QE.%d.%d" % (t, h))
            if h == 0:
                S["ec", t] = ecp.tile([P, 512], U32, name="ec", align_bytes=64)
                S["es", t] = ecp.tile([P, 512], U8, name="es", align_bytes=64)
            w = slice(h * 256, (h + 1) * 256)
            nc.vector.quantize_mx(out=S["ec", t][:, w].bitcast(FP8X4), scales=S["es", t][:, w], in_=S["ge", t][:, h * 1024:(h + 1) * 1024])

        def OR(b):
            mark("OR.%d" % b)
            S["ri", b] = const.tile([P, 4], F32, name="ri%d" % b)
            nc.vector.reciprocal(out=S["ri", b][:], in_=S["rs", b][:])

        def M2(t, gs=range(4)):
            mark("M2.%d" % t)
            b, qt = divmod(t, 4)
            for g in gs:
                if g == 0:
                    S["po", t] = ps_acc.tile([P, H], F32, name="acc")
                nc.tensor.matmul_mx(S["po", t][:], lhsT=S["ec", t][:, g * P:(g + 1) * P].bitcast(FP8X4), lhsT_scale=S["es", t][:, g * P:(g + 1) * P],
                                    rhs=S["vc", b][:, g * H:(g + 1) * H].bitcast(FP8X4), rhs_scale=S["vs", b][:, g * H:(g + 1) * H],
                                    start=(g == 0), stop=(g == 3))

        def OM(t, eng="s"):
            mark("OM.%d.%s" % (t, eng))
            b, qt = divmod(t, 4)
            o = op.tile([P, H], F32, name="o")
            if eng == "v":
                nc.vector.tensor_scalar_mul(out=o[:], in0=S["po", t][:], scalar1=S["ri", b][:, qt:qt + 1])
            else:
                nc.scalar.activation(out=o[:], in_=S["po", t][:], func=ACT.Copy, scale=S["ri", b][:, qt:qt + 1])
            mark("OS.%d" % t)
            nc.sync.dma_start(out=out[b].rearrange("(p t) h -> t p h", t=4)[qt], in_=o[:])

        def XT(c, t):
            mark("XT.%d.%d" % (c, t))
            px = ps_tp.tile([P, 512], F32, name="tp")
            S["px", c, t] = px
            src = S["xr", c][:].bitcast(F32)
            for i in range(4):
                nc.tensor.transpose(px[:, i * P:(i + 1) * P], src[:, t * 512 + i * P:t * 512 + (i + 1) * P], S["idf"][:])

        def XE(c, t):
            mark("XE.%d.%d.s" % (c, t))
            if t == 0:
                S["gx", c] = gxp.tile([P, 4096], BF16, name="gx", align_bytes=64)
            dst = S["gx", c][:].bitcast(F32)[:, t * 512:(t + 1) * 512].rearrange("p (g k u) -> p g k u", g=2, u=2)
            src = S["px", c, t][:].rearrange("p (g u k) -> p g k u", g=2, u=2)
            nc.scalar.copy(out=dst, in_=src)

        def QX(c):
            mark("QX.%d" % c)
            xc = gxp.tile([P, 1024], U32, name="xc", align_bytes=64)
            xs = gxp.tile([P, 1024], U8, name="xs", align_bytes=64)
            S["xc", c], S["xs", c] = xc, xs
            nc.vector.quantize_mx(out=xc[:].bitcast(FP8X4), scales=xs[:], in_=S["gx", c][:])

        def M1(c, hh):
            mark("M1.%d.%d" % (c, hh))
            xc, xs, wc, ws = S["xc", c], S["xs", c], S["wc"], S["ws"]
            pv = ps_acc.tile([P, 512], F32, name="acc")
            S["pv", c, hh] = pv
            for t in range(4):
                for gd in range(2):
                    a = t * 256 + gd * P
                    w0 = gd * H + hh * P
                    nc.tensor.matmul_mx(pv[:, t * P:(t + 1) * P], lhsT=xc[:, a:a + P].bitcast(FP8X4), lhsT_scale=xs[:, a:a + P],
                                        rhs=wc[:, w0:w0 + P].bitcast(FP8X4), rhs_scale=ws[:, w0:w0 + P],
                                        start=(gd == 0), stop=(gd == 1))

        def VE(c):
            gv = gvp.tile([P, 1024], BF16, name="gv", align_bytes=64)
            S["gv", c] = gv
            for hh in range(2):
                mark("VE.%d.%d" % (c, hh))
                nc.vector.tensor_tensor(out=gv[:, hh * 512:(hh + 1) * 512].rearrange("p (h t) -> p h t", t=4),
                                        in0=S["pv", c, hh][:].rearrange("p (t h) -> p h t", t=4),
                                        in1=S["row"][:, hh * P:(hh + 1) * P].unsqueeze(2).to_broadcast([P, P, 4]), op=ALU.add)

        def QV(c):
            mark("QV.%d" % c)
            b, g = divmod(c, 4)
            if g == 0:
                S["vc", b] = vcp.tile([P, 4 * H], U32, name="vc", align_bytes=64)
                S["vs", b] = vcp.tile([P, 4 * H], U8, name="vs", align_bytes=64)
            nc.vector.quantize_mx(out=S["vc", b][:, g * H:(g + 1) * H].bitcast(FP8X4), scales=S["vs", b][:, g * H:(g + 1) * H], in_=S["gv", c][:])

        consts()
        first = load_pi(0, 2)
        first(0)
        load_q(0)
        first(1)
        load_k(0, 0)
        load_k(0, 1)
        load_pi(1)(0)
        load_k(0, 2)
        load_k(0, 3)
        load_pi(2)(0)
        load_pi(3)(0)
        for i in range(2):
            LN(0, i, 2)
            Fl(0, i, 2)
        for j in range(3):
            KT(0, j)
            KE(0, j, "v")
        spread_row()
        for i in range(2):
            LG(0, i)
        for j in range(3, 5):
            KT(0, j)
        for i in range(2):
            Z(0, i)
        for j in range(3, 5):
            KE(0, j, "v")
        for i in range(2, 4):
            LG(0, i)
        for t in range(1, N_TILES):
            if t >= 4:
                load_pi(t)(0)
            LN(t)
            for i in range(1):
                Fl(t, i, 1)
            if t == 3:
                load_q(1)
            if t == 4:
                for j in range(4):
                    load_k(1, j)
            if t == 5:
                load_w()
                w_group()
        for c in range(4):
            load_x(c)

        units = []
        for t in range(PRE, N_TILES):
            units += [(t, 0), (t, 1), (t, 2)]
        done = [0, 0]

        def unit():
            if done[0] < len(units):
                t, k = units[done[0]]
                done[0] += 1
                if k < 2:
                    Z(t, 2 * k)
                    Z(t, 2 * k + 1)
                else:
                    MR(t)

        def upcoming(n):
            want = sum(1 for t, k in units[:done[0] + n] if k < 2)
            while done[1] < want:
                t, half = PRE + done[1] // 2, done[1] % 2
                LG(t, 2 * half)
                LG(t, 2 * half + 1)
                done[1] += 1

        for t in range(PRE):
            for i in range(2 if t == 0 else 1, 4):
                Z(t, i)
            if t == 2:
                for j in range(4):
                    KT(1, j)
            if t + 1 < PRE:
                for i in range(4):
                    LG(t + 1, i)
                Z(t + 1, 0)
            if t == 2:
                KE(1, 0, "v")
                KT(1, 4)
                for j in range(1, 5):
                    KE(1, j, "s")
            MR(t)
            if t == PRE - 2:
                for c in range(2):
                    for i in range(4):
                        XT(c, i)
                    for i in range(4):
                        XE(c, i)
                for i in range(2):
                    XT(2, i)

        w_quant()
        load_x(4)
        upcoming(2)
        QX(0)

        for r in range(N_TILES):
            last = r == N_TILES - 1
            if not last:
                EX(r)
            if not last and r >= 2:
                QX(r + 1)
            unit()
            if r >= 1:
                QV(r - 1)
            unit()
            if r < 2:
                QX(r + 1)
            if last:
                EX_half(r, 0)
                EX_half(r, 1)
            if r >= 1:
                EV(r - 1, 0, "s" if r - 1 < 8 else "v")
                EV(r - 1, 1, "s" if r - 1 < 8 else "v")
            if r >= 6:
                OM(2 * r - 12, "s")
                OM(2 * r - 11, "s")

            if r < 2:
                M1(r, 0)
                M1(r, 1)
            if r + 2 < N_CHUNKS:
                XT(r + 2, 2)
                XT(r + 2, 3)
                for i in range(4):
                    XE(r + 2, i)
                if r + 5 < N_CHUNKS:
                    load_x(r + 5)
            if r >= 6:
                ET(r, 0)
                if not last:
                    ET(r, 1)
            if r >= 2:
                M1(r, 0)
                M1(r, 1)
            if 5 <= r < 7:
                M2(2 * r - 10)
                M2(2 * r - 9)
            if r < 6:
                ET(r, 0)
                ET(r, 1)
            if last:
                ET(r, 1)
                for t in range(4, 6):
                    M2(t, range(3))
            VE(r)
            if 1 <= r:
                QE(r - 1)
            if r == 4:
                OR(0)
            if last:
                QV(r)
            if last:
                break
            if r + 3 < N_CHUNKS:
                XT(r + 3, 0)
                XT(r + 3, 1)
            upcoming(2)
        RS(7)
        EV(7, 0, "s")
        OR(1)
        M2(4, range(3, 4))
        M2(5, range(3, 4))
        M2(6)
        QE_half(7, 0)
        EV(7, 1, "s")
        QE_half(7, 1)
        for t in (4, 5, 6):
            OM(t)
        M2(7)
        OM(7)
